import numpy as np
import ml_dtypes


def mxq(x, axis, fmt="e4m3"):
    dtype, down = {"e4m3": (ml_dtypes.float8_e4m3fn, 7), "e5m2": (ml_dtypes.float8_e5m2, 14)}[fmt]
    v = np.moveaxis(np.asarray(x, np.float32).astype(ml_dtypes.bfloat16).astype(np.float64), axis, -1)
    blocks = v.reshape(v.shape[:-1] + (-1, 32))
    amax = np.abs(blocks).max(-1, keepdims=True)
    byte = np.maximum(np.where(amax > 0, np.frexp(amax)[1] - 1 + 127, 0) - down, 1)
    scale = np.exp2(byte - 127.0)
    codes = (blocks / scale).astype(np.float32).astype(dtype).astype(np.float64)
    return np.moveaxis((codes * scale).reshape(v.shape), -1, axis)


WIDE = False


def mx_kscale(k):
    if not WIDE:
        return np.ones(k)
    levels = np.array([10, -10, 5, -5, 0])
    if k % 512:
        return np.exp2(np.random.permutation(np.resize(levels, k // 32))).repeat(32)
    a = np.empty((k // 512, 16))
    for p in range(k // 512):
        a[p, :8] = np.random.permutation(np.resize(levels, 8))
        for g in range(8):
            far = levels[np.abs(levels - a[p, g]) >= 10]
            a[p, g + 8] = far[np.random.randint(len(far))]
    return np.exp2(a.ravel()).repeat(32)


BF16 = ml_dtypes.bfloat16


def bf(x):
    return np.asarray(x, np.float32).astype(BF16)


def f64(x):
    return np.asarray(x).astype(np.float64)


D, KW, STRIDE, STACK, B, O = 32, 11, 3, 16, 4096, 128
W_IN = D * D
POS = (D - KW) // STRIDE + 1
K = STACK * POS * POS


def build_mask():
    base_new = np.tile(np.arange(KW), KW)
    addition_new = np.repeat(np.arange(KW) * D, KW)
    index_1 = addition_new + base_new
    index_width = np.tile(index_1, POS)
    addition_width = np.repeat(STRIDE * np.arange(POS), KW * KW)
    index_row = index_width + addition_width
    index_column = np.tile(index_row, POS)
    addition_height = np.repeat(STRIDE * D * np.arange(POS), KW * KW * POS)
    index_final = index_column + addition_height
    stack = np.repeat(np.arange(POS * POS), KW * KW)
    block = np.zeros((POS * POS, W_IN))
    block[stack, index_final] = 1.0
    return np.vstack([block] * STACK)


def setup_inputs():
    s, t = mx_kscale(W_IN), mx_kscale(K)
    return {"z": bf(np.random.standard_normal((B, W_IN)) * s),
            "T3": bf(np.random.standard_normal((K, W_IN)) * 0.7 / np.sqrt(KW * KW) / s),
            "mask": bf(build_mask()),
            "x1": bf(np.random.standard_normal((B, K)) * 0.7 * t),
            "x2": bf(np.random.standard_normal((B, K)) * 1.4 * t),
            "C_w": bf(np.random.standard_normal((O, K)) / np.sqrt(K) / t),
            "C_b": bf(np.random.standard_normal(O) * 0.5)}


def reference(z, T3, mask, x1, x2, C_w, C_b):
    zq = mxq(f64(z).reshape(-1, D * D), 1, "e4m3")
    p3 = zq @ mxq(f64(mask) * f64(T3), 1, "e4m3").T
    x3 = 2.0 * p3 * f64(x2) - f64(x1)
    return (mxq(x3, 1, "e4m3") @ mxq(f64(C_w), 1, "e4m3").T) + f64(C_b)

@@ -1,0 +1,363 @@
+from contextlib import ExitStack
+
+import concourse.mybir as mybir
+from concourse.masks import make_identity
+
+F32 = mybir.dt.float32
+BF16 = mybir.dt.bfloat16
+U32 = mybir.dt.uint32
+U8 = mybir.dt.uint8
+FP8X4 = mybir.dt.float8_e4m3fn_x4
+ALU = mybir.AluOpType
+
+P = 128
+B, KIN, F, O = 4096, 1024, 1024, 128
+NCH = 8
+NPAIR = 16
+FLOPS = 2 * B * KIN * F + 2 * B * F * O
+
+N_PLAIN = 6
+GP_SHORT = 704
+GP_LONG = 960
+G_OF_PR = [[0], [0, 1], [0, 1], [1]]
+CI = {(0, 0): 0, (1, 0): 1, (2, 0): 2, (1, 1): 5, (2, 1): 6, (3, 1): 7}
+
+
+def tile_chebyshev_l3_sparsed32_stack_pb_t_kernel(tc, z, T3, mask, x1, x2, C_w, C_b, out):
+    nc = tc.nc
+    with ExitStack() as ctx:
+        const = ctx.enter_context(tc.tile_pool(name="const", bufs=1))
+        stream = ctx.enter_context(tc.tile_pool(name="stream", bufs=4))
+        work = ctx.enter_context(tc.tile_pool(name="work", bufs=3))
+        psum = ctx.enter_context(tc.psum_pool(name="psum", bufs=1))
+        ctx.enter_context(tc.manual_schedule())
+
+        zv = z.rearrange("(c p j) k -> c p (j k)", p=P, j=4)
+        x1v = x1.rearrange("(c p j) k -> c p (j k)", p=P, j=4)
+        x2v = x2.rearrange("(c p j) k -> c p (j k)", p=P, j=4)
+        outv = out.rearrange("(c p j) o -> c p (j o)", p=P, j=4)
+        t3v = T3.rearrange("(ft q) k -> q ft k", q=P)
+        mkv = mask.rearrange("(ft q) k -> q ft k", q=P)
+
+        ident_f = const.tile([P, P], F32, name="ident_f")
+        make_identity(nc, ident_f[:])
+        ident_b = const.tile([P, P], BF16, name="ident_b")
+        make_identity(nc, ident_b[:])
+
+        z_sb = {}
+        x1_sb = {}
+        x2_sb = {}
+        PW = 2 * KIN
+
+        def load_half(dst, src, c, hf, tag):
+            t = stream.tile([P, PW], BF16, name="%s_%d_%d" % (tag, c, hf), tag=tag)
+            nc.sync.dma_start(out=t[:], in_=src[c][:, hf * PW:(hf + 1) * PW])
+            dst[2 * c + hf] = t[:]
+
+        def load_whole(dst, src, c, tag):
+            t = stream.tile([P, 2 * PW], BF16, name="%s_%d" % (tag, c), tag=tag)
+            nc.sync.dma_start(out=t[:], in_=src[c])
+            for hf in range(2):
+                dst[2 * c + hf] = t[:, hf * PW:(hf + 1) * PW]
+
+        load_half(z_sb, zv, 0, 0, "z")
+        t3h = []
+        mkh = []
+        for hh in range(2):
+            t3_t = stream.tile([P, 4 * KIN], BF16, name="t3_%d" % hh, tag="x1")
+            mk_t = stream.tile([P, 4 * KIN], BF16, name="mk_%d" % hh, tag="x2")
+            t3h.append(t3_t)
+            mkh.append(mk_t)
+        for fp in range(4):
+            hh, lo = fp // 2, (fp % 2) * 2 * KIN
+            nc.sync.dma_start(
+                out=t3h[hh][:, lo:lo + 2 * KIN].rearrange("p (f k) -> p f k", f=2),
+                in_=t3v[:, 2 * fp:2 * fp + 2, :])
+            nc.sync.dma_start(
+                out=mkh[hh][:, lo:lo + 2 * KIN].rearrange("p (f k) -> p f k", f=2),
+                in_=mkv[:, 2 * fp:2 * fp + 2, :])
+        c_sb = const.tile([P, F], BF16, name="c_sb")
+        nc.scalar.dma_start(out=c_sb[:], in_=C_w)
+        bias_sb = const.tile([P, O], BF16, name="bias_sb")
+        nc.scalar.dma_start(out=bias_sb[:], in_=C_b.partition_broadcast(P))
+        load_half(x2_sb, x2v, 0, 0, "x2")
+        load_half(z_sb, zv, 0, 1, "z")
+        load_half(z_sb, zv, 1, 0, "z")
+        load_half(x1_sb, x1v, 0, 0, "x1")
+        load_half(x2_sb, x2v, 0, 1, "x2")
+        load_half(x1_sb, x1v, 0, 1, "x1")
+        load_half(z_sb, zv, 1, 1, "z")
+        load_half(x2_sb, x2v, 1, 0, "x2")
+        load_half(x1_sb, x1v, 1, 0, "x1")
+        load_whole(z_sb, zv, 2, "z")
+        load_half(x2_sb, x2v, 1, 1, "x2")
+        load_half(x1_sb, x1v, 1, 1, "x1")
+        load_whole(z_sb, zv, 3, "z")
+        later_loads = {1: (2, 4), 2: (3, 5), 3: (4, 6), 4: (5, None), 5: (None, 7), 6: (6, None), 8: (7, None)}
+
+        zg = {}
+        zc = {}
+        zs = {}
+
+        def z_t(k, g, early=False):
+            if g == 0:
+                zg[k] = work.tile([P, 2 * 256 * 4], BF16, name="zg_%d" % k, tag="zg", align_bytes=64)
+            zw = z_sb[k].bitcast(F32)
+            zt = psum.tile([P, 2, 256], F32, name="zt", tag=("p3" if early else "tp"), bufs=(5 if early else 1))
+            for u in range(2):
+                for jl in range(2):
+                    col = jl * 512 + 256 * g
+                    nc.tensor.transpose(zt[:, u, jl * P:(jl + 1) * P], zw[:, col + u:col + 256:2], ident_f[:])
+            zgw = zg[k][:].bitcast(F32).rearrange("p (g c u) -> p g c u", g=2, u=2)
+            nc.scalar.copy(out=zgw[:, g, :, :], in_=zt[:].rearrange("p u c -> p c u"))
+
+        def z_q(k):
+            zc[k] = work.tile([P, 512], U32, name="zc_%d" % k, tag="zc", bufs=4, align_bytes=64)
+            zs[k] = work.tile([P, 512], U8, name="zs_%d" % k, tag="zs", bufs=4, align_bytes=64)
+            nc.vector.quantize_mx(out=zc[k][:].bitcast(FP8X4), scales=zs[k][:], in_=zg[k][:])
+
+        wg = const.tile([P, 8 * 256 * 4], BF16, name="wg", align_bytes=64)
+        wc = const.tile([P, 8 * 256], U32, name="wc", align_bytes=64)
+        ws = const.tile([P, 8 * 256], U8, name="ws", align_bytes=64)
+        wgw = wg[:].bitcast(F32).rearrange("p (g pr s r u) -> p g s pr r u", g=2, pr=4, s=16, r=16, u=2)
+
+        def w_mul(fp, parts):
+            hh, lo = fp // 2, (fp % 2) * 2 * KIN
+            tv = t3h[hh][:, lo:lo + 2 * KIN].rearrange("p (f k) -> p f k", f=2)
+            mv = mkh[hh][:, lo:lo + 2 * KIN].rearrange("p (f k) -> p f k", f=2)
+            w = KIN // parts
+            for i in range(parts):
+                nc.vector.tensor_tensor(
+                    out=tv[:, :, i * w:(i + 1) * w], in0=tv[:, :, i * w:(i + 1) * w],
+                    in1=mv[:, :, i * w:(i + 1) * w], op=ALU.mult)
+
+        def w_t(fp, second_on_vector):
+            hh, lo = fp // 2, (fp % 2) * 2 * KIN
+            ww = t3h[hh][:].bitcast(F32)
+            for g in range(2):
+                wt = psum.tile([P, 2, 256], F32, name="wt", tag="p3", bufs=5)
+                for u in range(2):
+                    for fl in range(2):
+                        col = lo // 2 + fl * 512 + 256 * g
+                        nc.tensor.transpose(wt[:, u, fl * P:(fl + 1) * P], ww[:, col + u:col + 256:2], ident_f[:])
+                src = wt[:].rearrange("p u (s pr r) -> p s pr r u", s=4, pr=4, r=16)
+                dst = wgw[:, g, 4 * fp:4 * fp + 4, :, :, :]
+                if g == 1 and second_on_vector:
+                    nc.vector.tensor_copy(out=dst, in_=src)
+                else:
+                    nc.scalar.copy(out=dst, in_=src)
+
+        def w_q(fp):
+            for pr in range(4):
+                for g in G_OF_PR[pr]:
+                    lo_w = CI[(pr, g)] * 256 + 64 * fp
+                    nc.vector.quantize_mx(
+                        out=wc[:, lo_w:lo_w + 64].bitcast(FP8X4), scales=ws[:, lo_w:lo_w + 64],
+                        in_=wg[:, 4 * lo_w:4 * lo_w + 256])
+
+        cg = const.tile([P, 2 * O * 4], BF16, name="cg", align_bytes=64)
+        cc = const.tile([P, 2 * O], U32, name="cc", align_bytes=64)
+        cs = const.tile([P, 2 * O], U8, name="cs", align_bytes=64)
+
+        cp = const.tile([P, F], BF16, name="cp")
+
+        def c_t():
+            nc.scalar.copy(
+                out=cp[:].rearrange("p (g t q i) -> p g t q i", g=2, t=4, i=4),
+                in_=c_sb[:].rearrange("p (g q t i) -> p g t q i", g=2, t=4, i=4))
+            ct = psum.tile([P, 8, P], BF16, name="ct", tag="xt", bufs=1)
+            for gt in range(8):
+                nc.tensor.transpose(ct[:, gt, :], cp[:, gt * P:(gt + 1) * P], ident_b[:])
+            nc.scalar.copy(
+                out=cg[:].rearrange("p (g o t) -> p g o t", g=2, t=4),
+                in_=ct[:].rearrange("p (g t) o -> p g o t", g=2))
+
+        def c_q():
+            nc.vector.quantize_mx(out=cc[:].bitcast(FP8X4), scales=cs[:], in_=cg[:])
+
+        p3 = {}
+        y_sb = {}
+        x3_sb = {}
+        xg = {}
+        xc = {}
+        xs = {}
+        po = {}
+
+        def mm1(k, pr):
+            bank = psum.tile([P, 512], F32, name="p3_%d_%d" % (k, pr), tag="p3", bufs=5)
+            p3[(k, pr)] = bank
+            gs = G_OF_PR[pr]
+            for jl in range(2):
+                for g in gs:
+                    lo = g * 256 + jl * P
+                    ci = CI[(pr, g)]
+                    nc.tensor.matmul_mx(
+                        out=bank[:, jl * 256:(jl + 1) * 256],
+                        lhsT=zc[k][:, lo:lo + P].bitcast(FP8X4), lhsT_scale=zs[k][:, lo:lo + P],
+                        rhs=wc[:, ci * 256:(ci + 1) * 256].bitcast(FP8X4), rhs_scale=ws[:, ci * 256:(ci + 1) * 256],
+                        start=(g == gs[0]), stop=(g == gs[-1]))
+
+        def op1(k):
+            y_sb[k] = work.tile([P, PW], F32, name="y_%d" % k, tag="y")
+            yv = y_sb[k][:].rearrange("p (s q) -> p s q", q=64)
+            x2u = x2_sb[k].rearrange("p (s q) -> p s q", q=64)
+            for pr in range(4):
+                nc.vector.scalar_tensor_tensor(
+                    out=yv[:, :, pr * 16:(pr + 1) * 16],
+                    in0=p3[(k, pr)][:].rearrange("p (s r) -> p s r", r=16),
+                    scalar=2.0,
+                    in1=x2u[:, :, pr * 16:(pr + 1) * 16],
+                    op0=ALU.mult, op1=ALU.mult)
+
+        def op2(k, lo, hi, eng):
+            if k not in x3_sb:
+                x3_sb[k] = work.tile([P, PW], BF16, name="x3_%d" % k, tag="x3", bufs=4)
+            q = slice(lo // 16, hi // 16)
+            x1p = x1_sb[k].rearrange("p (q t i) -> p t q i", t=4, i=4)
+            yp = y_sb[k][:].rearrange("p (q t i) -> p t q i", t=4, i=4)
+            xp = x3_sb[k][:].rearrange("p (t q i) -> p t q i", t=4, i=4)
+            eng.tensor_tensor(out=xp[:, :, q, :], in0=yp[:, :, q, :], in1=x1p[:, :, q, :], op=ALU.subtract)
+
+        def x_t(k, unit, tail=False, split=False):
+            if unit == 0:
+                xg[k] = work.tile([P, 2 * 1024], BF16, name="xg_%d" % k, tag="xg", bufs=4, align_bytes=64)
+            dst = xg[k][:, unit * 1024:(unit + 1) * 1024].rearrange("p (g b t) -> p g b t", g=2, t=4)
+            if split:
+                for g in range(2):
+                    xh = psum.tile([P, 4, P], BF16, name="xh", tag="p3", bufs=5)
+                    for t in range(4):
+                        col = t * 512 + unit * 256 + g * P
+                        nc.tensor.transpose(xh[:, t, :], x3_sb[k][:, col:col + P], ident_b[:])
+                    if g == 0:
+                        nc.scalar.copy(out=dst[:, g], in_=xh[:].rearrange("p t b -> p b t"))
+                    else:
+                        nc.vector.tensor_copy(out=dst[:, g], in_=xh[:].rearrange("p t b -> p b t"))
+            else:
+                xt = psum.tile([P, 8, P], BF16, name="xt", tag=("p3" if tail else "xt"), bufs=(5 if tail else 1))
+                for gt in range(8):
+                    col = (gt % 4) * 512 + unit * 256 + (gt // 4) * P
+                    if gt < N_PLAIN:
+                        nc.tensor.matmul(
+                            out=xt[:, gt, :], lhsT=x3_sb[k][:, col:col + P], rhs=ident_b[:], start=True, stop=True)
+                    else:
+                        nc.tensor.transpose(xt[:, gt, :], x3_sb[k][:, col:col + P], ident_b[:])
+                nc.scalar.copy(out=dst, in_=xt[:].rearrange("p (g t) b -> p g b t", g=2))
+
+        def x_q(k, units):
+            if k not in xc:
+                xc[k] = work.tile([P, 512], U32, name="xc_%d" % k, tag="xc", align_bytes=64)
+                xs[k] = work.tile([P, 512], U8, name="xs_%d" % k, tag="xs", align_bytes=64)
+            lo, n = units[0] * 256, len(units) * 256
+            nc.vector.quantize_mx(
+                out=xc[k][:, lo:lo + n].bitcast(FP8X4), scales=xs[k][:, lo:lo + n], in_=xg[k][:, 4 * lo:4 * (lo + n)])
+
+        def mm2(k, units):
+            c = k // 2
+            if c not in po:
+                po[c] = psum.tile([P, 4, O], F32, name="po_%d" % c, tag="po", bufs=1)
+            for unit in units:
+                for g in range(2):
+                    lo = (unit * 2 + g) * P
+                    nc.tensor.matmul_mx(
+                        out=po[c][:, (k % 2) * 2 + unit, :],
+                        lhsT=xc[k][:, lo:lo + P].bitcast(FP8X4), lhsT_scale=xs[k][:, lo:lo + P],
+                        rhs=cc[:, g * O:(g + 1) * O].bitcast(FP8X4), rhs_scale=cs[:, g * O:(g + 1) * O],
+                        start=(g == 0), stop=(g == 1))
+
+        def fin(c):
+            o_sb = work.tile([P, 4, O], F32, name="o_sb", tag="o_sb", bufs=2)
+            nc.vector.tensor_tensor(
+                out=o_sb[:], in0=po[c][:], in1=bias_sb[:].unsqueeze(1).to_broadcast([P, 4, O]), op=ALU.add)
+            nc.sync.dma_start(out=outv[c], in_=o_sb[:].rearrange("p j o -> p (j o)"))
+
+        mark = const.tile([P, 1], BF16, name="mark")
+        BOTH = [0, 1]
+
+        def gp_cols(k):
+            return GP_LONG if ((k + 1) % 2 == 0 and k + 1 >= 6) else GP_SHORT
+        z_t(0, 0, True)
+        z_t(0, 1, True)
+        z_q(0)
+        c_t()
+        c_q()
+        w_mul(0, 1)
+        w_t(0, False)
+        w_mul(1, 1)
+        w_t(1, False)
+        w_mul(2, 1)
+        w_q(0)
+        w_t(2, False)
+        w_q(1)
+        w_mul(3, 2)
+        w_q(2)
+        w_t(3, True)
+        w_q(3)
+        z_t(1, 0)
+        z_t(1, 1, True)
+        for pr in range(4):
+            mm1(0, pr)
+        z_t(2, 0)
+        z_t(2, 1)
+
+        for k in range(NPAIR):
+            last = k == NPAIR - 1
+            if k >= 1:
+                nc.gpsimd.tensor_copy(out=mark[:], in_=x3_sb[k - 1][:, 256:257])
+                op2(k - 1, 0, gp_cols(k - 1), nc.gpsimd)
+            if k in later_loads:
+                cx, cz = later_loads[k]
+                if cx is not None:
+                    load_whole(x2_sb, x2v, cx, "x2")
+                    load_whole(x1_sb, x1v, cx, "x1")
+                if cz is not None:
+                    load_whole(z_sb, zv, cz, "z")
+            if k >= 6 and k % 2 == 0:
+                fin((k - 6) // 2)
+            if k == 0:
+                op1(0)
+                z_q(1)
+            if not last:
+                mm1(k + 1, 0)
+                mm1(k + 1, 1)
+            if k >= 2:
+                x_t(k - 2, 0)
+            if k + 3 < NPAIR:
+                z_t(k + 3, 0)
+            if not last:
+                mm1(k + 1, 2)
+                mm1(k + 1, 3)
+            if k >= 4:
+                mm2(k - 4, BOTH)
+            if k >= 2:
+                x_t(k - 2, 1)
+            if k + 3 < NPAIR:
+                z_t(k + 3, 1)
+            if k >= 1:
+                op1(k)
+            if last:
+                op2(k, 0, F, nc.vector)
+                op2(k, F, PW, nc.vector)
+            else:
+                if k >= 3:
+                    x_q(k - 3, BOTH)
+                if k + 2 < NPAIR:
+                    z_q(k + 2)
+                op2(k, gp_cols(k), PW, nc.vector)
+
+        x_t(NPAIR - 2, 0, True)
+        x_t(NPAIR - 2, 1, True)
+        x_t(NPAIR - 1, 0, True)
+        x_t(NPAIR - 1, 1, True, True)
+        x_q(NPAIR - 4, BOTH)
+        fin(NCH - 3)
+        mm2(NPAIR - 4, BOTH)
+        x_q(NPAIR - 3, BOTH)
+        mm2(NPAIR - 3, BOTH)
+        x_q(NPAIR - 2, BOTH)
+        fin(NCH - 2)
+        mm2(NPAIR - 2, BOTH)
+        x_q(NPAIR - 1, [0])
+        mm2(NPAIR - 1, [0])
+        x_q(NPAIR - 1, [1])
+        mm2(NPAIR - 1, [1])
+        fin(NCH - 1)

@@ -37,7 +37,6 @@ def tile_chebyshev_l3_sparsed32_stack_pb_t_kernel(tc, z, T3, mask, x1, x2, C_w, 
         x2v = x2.rearrange("(c p j) k -> c p (j k)", p=P, j=4)
         outv = out.rearrange("(c p j) o -> c p (j o)", p=P, j=4)
         t3v = T3.rearrange("(ft q) k -> q ft k", q=P)
-        mkv = mask.rearrange("(ft q) k -> q ft k", q=P)
 
         ident_f = const.tile([P, P], F32, name="ident_f")
         make_identity(nc, ident_f[:])
@@ -60,26 +59,27 @@ def tile_chebyshev_l3_sparsed32_stack_pb_t_kernel(tc, z, T3, mask, x1, x2, C_w, 
             for hf in range(2):
                 dst[2 * c + hf] = t[:, hf * PW:(hf + 1) * PW]
 
-        load_half(z_sb, zv, 0, 0, "z")
+        mk_sb = const.tile([P, KIN], BF16, name="mk_sb")
+        nc.sync.dma_start(out=mk_sb[:], in_=mask[0:P, :])
         t3h = []
-        mkh = []
         for hh in range(2):
             t3_t = stream.tile([P, 4 * KIN], BF16, name="t3_%d" % hh, tag="x1")
-            mk_t = stream.tile([P, 4 * KIN], BF16, name="mk_%d" % hh, tag="x2")
             t3h.append(t3_t)
-            mkh.append(mk_t)
         for fp in range(4):
             hh, lo = fp // 2, (fp % 2) * 2 * KIN
             nc.sync.dma_start(
                 out=t3h[hh][:, lo:lo + 2 * KIN].rearrange("p (f k) -> p f k", f=2),
                 in_=t3v[:, 2 * fp:2 * fp + 2, :])
-            nc.sync.dma_start(
-                out=mkh[hh][:, lo:lo + 2 * KIN].rearrange("p (f k) -> p f k", f=2),
-                in_=mkv[:, 2 * fp:2 * fp + 2, :])
+            if fp == 1:
+                load_half(z_sb, zv, 0, 0, "z")
         c_sb = const.tile([P, F], BF16, name="c_sb")
         nc.scalar.dma_start(out=c_sb[:], in_=C_w)
-        bias_sb = const.tile([P, O], BF16, name="bias_sb")
-        nc.scalar.dma_start(out=bias_sb[:], in_=C_b.partition_broadcast(P))
+        bias_row = const.tile([P, O], BF16, name="bias_row")
+        nc.gpsimd.memset(bias_row[:], 0.0)
+        nc.scalar.dma_start(out=bias_row[0:1, :], in_=C_b.unsqueeze(0))
+        ones = const.tile([P, P], BF16, name="ones")
+        nc.gpsimd.memset(ones[:], 1.0)
+        bias_sb = const.tile([P, O], F32, name="bias_sb")
         load_half(x2_sb, x2v, 0, 0, "x2")
         load_half(z_sb, zv, 0, 1, "z")
         load_half(z_sb, zv, 1, 0, "z")
@@ -99,11 +99,12 @@ def tile_chebyshev_l3_sparsed32_stack_pb_t_kernel(tc, z, T3, mask, x1, x2, C_w, 
         zc = {}
         zs = {}
 
-        def z_t(k, g, early=False):
+        def z_t(k, g, early=None):
             if g == 0:
                 zg[k] = work.tile([P, 2 * 256 * 4], BF16, name="zg_%d" % k, tag="zg", align_bytes=64)
             zw = z_sb[k].bitcast(F32)
-            zt = psum.tile([P, 2, 256], F32, name="zt", tag=("p3" if early else "tp"), bufs=(5 if early else 1))
+            tag, bufs = early if early else ("tp", 1)
+            zt = psum.tile([P, 2, 256], F32, name="zt", tag=tag, bufs=bufs)
             for u in range(2):
                 for jl in range(2):
                     col = jl * 512 + 256 * g
@@ -121,25 +122,29 @@ def tile_chebyshev_l3_sparsed32_stack_pb_t_kernel(tc, z, T3, mask, x1, x2, C_w, 
         ws = const.tile([P, 8 * 256], U8, name="ws", align_bytes=64)
         wgw = wg[:].bitcast(F32).rearrange("p (g pr s r u) -> p g s pr r u", g=2, pr=4, s=16, r=16, u=2)
 
-        def w_mul(fp, parts):
+        wm = []
+
+        def w_mul(fp):
             hh, lo = fp // 2, (fp % 2) * 2 * KIN
-            tv = t3h[hh][:, lo:lo + 2 * KIN].rearrange("p (f k) -> p f k", f=2)
-            mv = mkh[hh][:, lo:lo + 2 * KIN].rearrange("p (f k) -> p f k", f=2)
-            w = KIN // parts
-            for i in range(parts):
-                nc.vector.tensor_tensor(
-                    out=tv[:, :, i * w:(i + 1) * w], in0=tv[:, :, i * w:(i + 1) * w],
-                    in1=mv[:, :, i * w:(i + 1) * w], op=ALU.mult)
+            if fp % 2 == 0:
+                wm_t = work.tile([P, PW], F32, name="wm_%d" % hh, tag="y")
+                wm.append(wm_t)
+            dst = wm[hh][:].bitcast(BF16)[:, lo:lo + 2 * KIN]
+            nc.vector.tensor_tensor(
+                out=dst.rearrange("p (u f m e) -> p f m u e", u=2, f=2, e=2),
+                in0=t3h[hh][:, lo:lo + 2 * KIN].rearrange("p (f m u e) -> p f m u e", f=2, u=2, e=2),
+                in1=mk_sb[:].rearrange("p (m u e) -> p m u e", u=2, e=2).unsqueeze(1).to_broadcast([P, 2, 256, 2, 2]),
+                op=ALU.mult)
 
         def w_t(fp, second_on_vector):
             hh, lo = fp // 2, (fp % 2) * 2 * KIN
-            ww = t3h[hh][:].bitcast(F32)
+            ww = wm[hh][:]
             for g in range(2):
                 wt = psum.tile([P, 2, 256], F32, name="wt", tag="p3", bufs=5)
                 for u in range(2):
                     for fl in range(2):
-                        col = lo // 2 + fl * 512 + 256 * g
-                        nc.tensor.transpose(wt[:, u, fl * P:(fl + 1) * P], ww[:, col + u:col + 256:2], ident_f[:])
+                        col = lo // 2 + u * 512 + fl * 256 + g * P
+                        nc.tensor.transpose(wt[:, u, fl * P:(fl + 1) * P], ww[:, col:col + P], ident_f[:])
                 src = wt[:].rearrange("p u (s pr r) -> p s pr r u", s=4, pr=4, r=16)
                 dst = wgw[:, g, 4 * fp:4 * fp + 4, :, :, :]
                 if g == 1 and second_on_vector:
@@ -161,10 +166,17 @@ def tile_chebyshev_l3_sparsed32_stack_pb_t_kernel(tc, z, T3, mask, x1, x2, C_w, 
 
         cp = const.tile([P, F], BF16, name="cp")
 
-        def c_t():
+        def bias_spread():
+            bt = psum.tile([P, O], F32, name="bt", tag="po", bufs=1)
+            nc.tensor.matmul(out=bt[:], lhsT=ones[:], rhs=bias_row[:], start=True, stop=True)
+            nc.scalar.copy(out=bias_sb[:], in_=bt[:])
+
+        def c_perm():
             nc.scalar.copy(
                 out=cp[:].rearrange("p (g t q i) -> p g t q i", g=2, t=4, i=4),
                 in_=c_sb[:].rearrange("p (g q t i) -> p g t q i", g=2, t=4, i=4))
+
+        def c_t():
             ct = psum.tile([P, 8, P], BF16, name="ct", tag="xt", bufs=1)
             for gt in range(8):
                 nc.tensor.transpose(ct[:, gt, :], cp[:, gt * P:(gt + 1) * P], ident_b[:])
@@ -197,16 +209,18 @@ def tile_chebyshev_l3_sparsed32_stack_pb_t_kernel(tc, z, T3, mask, x1, x2, C_w, 
                         rhs=wc[:, ci * 256:(ci + 1) * 256].bitcast(FP8X4), rhs_scale=ws[:, ci * 256:(ci + 1) * 256],
                         start=(g == gs[0]), stop=(g == gs[-1]))
 
-        def op1(k):
-            y_sb[k] = work.tile([P, PW], F32, name="y_%d" % k, tag="y")
+        def op1(k, units=(0, 1)):
+            if k not in y_sb:
+                y_sb[k] = work.tile([P, PW], F32, name="y_%d" % k, tag="y")
+            ss = slice(16 * units[0], 16 * units[-1] + 16)
             yv = y_sb[k][:].rearrange("p (s q) -> p s q", q=64)
             x2u = x2_sb[k].rearrange("p (s q) -> p s q", q=64)
             for pr in range(4):
                 nc.vector.scalar_tensor_tensor(
-                    out=yv[:, :, pr * 16:(pr + 1) * 16],
-                    in0=p3[(k, pr)][:].rearrange("p (s r) -> p s r", r=16),
+                    out=yv[:, ss, pr * 16:(pr + 1) * 16],
+                    in0=p3[(k, pr)][:].rearrange("p (s r) -> p s r", r=16)[:, ss, :],
                     scalar=2.0,
-                    in1=x2u[:, :, pr * 16:(pr + 1) * 16],
+                    in1=x2u[:, ss, pr * 16:(pr + 1) * 16],
                     op0=ALU.mult, op1=ALU.mult)
 
         def op2(k, lo, hi, eng):
@@ -253,51 +267,58 @@ def tile_chebyshev_l3_sparsed32_stack_pb_t_kernel(tc, z, T3, mask, x1, x2, C_w, 
 
         def mm2(k, units):
             c = k // 2
-            if c not in po:
-                po[c] = psum.tile([P, 4, O], F32, name="po_%d" % c, tag="po", bufs=1)
+            key = c if c < NCH - 1 else (k, units[0])
+            if key not in po:
+                po[key] = psum.tile([P, 4, O], F32, name="po_%d" % c,
+                                    tag=("po" if c < NCH - 1 else "p3"), bufs=(1 if c < NCH - 1 else 5))
             for unit in units:
                 for g in range(2):
                     lo = (unit * 2 + g) * P
                     nc.tensor.matmul_mx(
-                        out=po[c][:, (k % 2) * 2 + unit, :],
+                        out=po[key][:, (k % 2) * 2 + unit, :],
                         lhsT=xc[k][:, lo:lo + P].bitcast(FP8X4), lhsT_scale=xs[k][:, lo:lo + P],
                         rhs=cc[:, g * O:(g + 1) * O].bitcast(FP8X4), rhs_scale=cs[:, g * O:(g + 1) * O],
                         start=(g == 0), stop=(g == 1))
 
-        def fin(c):
+        def fin(c, key=None, lo=0, n=4):
             o_sb = work.tile([P, 4, O], F32, name="o_sb", tag="o_sb", bufs=2)
             nc.vector.tensor_tensor(
-                out=o_sb[:], in0=po[c][:], in1=bias_sb[:].unsqueeze(1).to_broadcast([P, 4, O]), op=ALU.add)
-            nc.sync.dma_start(out=outv[c], in_=o_sb[:].rearrange("p j o -> p (j o)"))
+                out=o_sb[:, lo:lo + n, :], in0=po[c if key is None else key][:, lo:lo + n, :],
+                in1=bias_sb[:].unsqueeze(1).to_broadcast([P, n, O]), op=ALU.add)
+            nc.sync.dma_start(out=outv[c][:, lo * O:(lo + n) * O],
+                              in_=o_sb[:, lo:lo + n, :].rearrange("p j o -> p (j o)"))
 
         mark = const.tile([P, 1], BF16, name="mark")
         BOTH = [0, 1]
 
         def gp_cols(k):
             return GP_LONG if ((k + 1) % 2 == 0 and k + 1 >= 6) else GP_SHORT
-        z_t(0, 0, True)
-        z_t(0, 1, True)
-        z_q(0)
-        c_t()
-        c_q()
-        w_mul(0, 1)
+        P3_BANK, X_BANK = ("p3", 5), ("xt", 1)
+        c_perm()
+        w_mul(0)
+        w_mul(1)
         w_t(0, False)
-        w_mul(1, 1)
+        z_t(0, 0, P3_BANK)
+        z_t(0, 1, P3_BANK)
+        w_mul(2)
         w_t(1, False)
-        w_mul(2, 1)
+        w_mul(3)
         w_q(0)
         w_t(2, False)
+        z_q(0)
         w_q(1)
-        w_mul(3, 2)
-        w_q(2)
+        c_t()
         w_t(3, True)
-        w_q(3)
+        w_q(2)
         z_t(1, 0)
-        z_t(1, 1, True)
+        w_q(3)
+        z_t(1, 1, P3_BANK)
+        bias_spread()
         for pr in range(4):
             mm1(0, pr)
         z_t(2, 0)
-        z_t(2, 1)
+        z_t(2, 1, X_BANK)
+        c_q()
 
         for k in range(NPAIR):
             last = k == NPAIR - 1
@@ -332,12 +353,16 @@ def tile_chebyshev_l3_sparsed32_stack_pb_t_kernel(tc, z, T3, mask, x1, x2, C_w, 
                 x_t(k - 2, 1)
             if k + 3 < NPAIR:
                 z_t(k + 3, 1)
-            if k >= 1:
-                op1(k)
             if last:
+                op1(k, [0])
+                op1(k, [1])
+                fin(NCH - 3)
                 op2(k, 0, F, nc.vector)
+                x_q(NPAIR - 4, BOTH)
                 op2(k, F, PW, nc.vector)
             else:
+                if k >= 1:
+                    op1(k)
                 if k >= 3:
                     x_q(k - 3, BOTH)
                 if k + 2 < NPAIR:
@@ -346,18 +371,18 @@ def tile_chebyshev_l3_sparsed32_stack_pb_t_kernel(tc, z, T3, mask, x1, x2, C_w, 
 
         x_t(NPAIR - 2, 0, True)
         x_t(NPAIR - 2, 1, True)
-        x_t(NPAIR - 1, 0, True)
-        x_t(NPAIR - 1, 1, True, True)
-        x_q(NPAIR - 4, BOTH)
-        fin(NCH - 3)
         mm2(NPAIR - 4, BOTH)
         x_q(NPAIR - 3, BOTH)
+        x_t(NPAIR - 1, 0, True)
         mm2(NPAIR - 3, BOTH)
         x_q(NPAIR - 2, BOTH)
+        x_t(NPAIR - 1, 1, True, True)
         fin(NCH - 2)
         mm2(NPAIR - 2, BOTH)
         x_q(NPAIR - 1, [0])
         mm2(NPAIR - 1, [0])
+        fin(NCH - 1, (NPAIR - 2, 0), 0, 2)
         x_q(NPAIR - 1, [1])
         mm2(NPAIR - 1, [1])
-        fin(NCH - 1)
+        fin(NCH - 1, (NPAIR - 1, 0), 2, 1)
+        fin(NCH - 1, (NPAIR - 1, 1), 3, 1)

@@ -73,17 +73,17 @@ def tile_chebyshev_l3_sparsed32_stack_pb_t_kernel(tc, z, T3, mask, x1, x2, C_w, 
             if fp == 1:
                 load_half(z_sb, zv, 0, 0, "z")
         c_sb = const.tile([P, F], BF16, name="c_sb")
-        nc.scalar.dma_start(out=c_sb[:], in_=C_w)
         bias_row = const.tile([P, O], BF16, name="bias_row")
         nc.gpsimd.memset(bias_row[:], 0.0)
-        nc.scalar.dma_start(out=bias_row[0:1, :], in_=C_b.unsqueeze(0))
         ones = const.tile([P, P], BF16, name="ones")
         nc.gpsimd.memset(ones[:], 1.0)
         bias_sb = const.tile([P, O], F32, name="bias_sb")
         load_half(x2_sb, x2v, 0, 0, "x2")
         load_half(z_sb, zv, 0, 1, "z")
         load_half(z_sb, zv, 1, 0, "z")
+        nc.sync.dma_start(out=c_sb[:], in_=C_w)
         load_half(x1_sb, x1v, 0, 0, "x1")
+        nc.sync.dma_start(out=bias_row[0:1, :], in_=C_b.unsqueeze(0))
         load_half(x2_sb, x2v, 0, 1, "x2")
         load_half(x1_sb, x1v, 0, 1, "x1")
         load_half(z_sb, zv, 1, 1, "z")
@@ -280,8 +280,10 @@ def tile_chebyshev_l3_sparsed32_stack_pb_t_kernel(tc, z, T3, mask, x1, x2, C_w, 
                         rhs=cc[:, g * O:(g + 1) * O].bitcast(FP8X4), rhs_scale=cs[:, g * O:(g + 1) * O],
                         start=(g == 0), stop=(g == 1))
 
+        o_last = const.tile([P, 4, O], F32, name="o_last")
+
         def fin(c, key=None, lo=0, n=4):
-            o_sb = work.tile([P, 4, O], F32, name="o_sb", tag="o_sb", bufs=2)
+            o_sb = o_last if key else work.tile([P, 4, O], F32, name="o_sb", tag="o_sb", bufs=2)
             nc.vector.tensor_tensor(
                 out=o_sb[:, lo:lo + n, :], in0=po[c if key is None else key][:, lo:lo + n, :],
                 in1=bias_sb[:].unsqueeze(1).to_broadcast([P, n, O]), op=ALU.add)
@@ -294,7 +296,6 @@ def tile_chebyshev_l3_sparsed32_stack_pb_t_kernel(tc, z, T3, mask, x1, x2, C_w, 
         def gp_cols(k):
             return GP_LONG if ((k + 1) % 2 == 0 and k + 1 >= 6) else GP_SHORT
         P3_BANK, X_BANK = ("p3", 5), ("xt", 1)
-        c_perm()
         w_mul(0)
         w_mul(1)
         w_t(0, False)
@@ -307,18 +308,16 @@ def tile_chebyshev_l3_sparsed32_stack_pb_t_kernel(tc, z, T3, mask, x1, x2, C_w, 
         w_t(2, False)
         z_q(0)
         w_q(1)
-        c_t()
         w_t(3, True)
         w_q(2)
-        z_t(1, 0)
+        z_t(1, 0, P3_BANK)
         w_q(3)
         z_t(1, 1, P3_BANK)
-        bias_spread()
-        for pr in range(4):
-            mm1(0, pr)
         z_t(2, 0)
         z_t(2, 1, X_BANK)
-        c_q()
+        for pr in range(4):
+            mm1(0, pr)
+        c_perm()
 
         for k in range(NPAIR):
             last = k == NPAIR - 1
@@ -340,6 +339,10 @@ def tile_chebyshev_l3_sparsed32_stack_pb_t_kernel(tc, z, T3, mask, x1, x2, C_w, 
             if not last:
                 mm1(k + 1, 0)
                 mm1(k + 1, 1)
+            if last:
+                mm2(k - 4, BOTH)
+            if k == 0:
+                c_t()
             if k >= 2:
                 x_t(k - 2, 0)
             if k + 3 < NPAIR:
@@ -347,8 +350,10 @@ def tile_chebyshev_l3_sparsed32_stack_pb_t_kernel(tc, z, T3, mask, x1, x2, C_w, 
             if not last:
                 mm1(k + 1, 2)
                 mm1(k + 1, 3)
-            if k >= 4:
+            if 4 <= k and not last:
                 mm2(k - 4, BOTH)
+            if k == 2:
+                bias_spread()
             if k >= 2:
                 x_t(k - 2, 1)
             if k + 3 < NPAIR:
@@ -356,13 +361,15 @@ def tile_chebyshev_l3_sparsed32_stack_pb_t_kernel(tc, z, T3, mask, x1, x2, C_w, 
             if last:
                 op1(k, [0])
                 op1(k, [1])
-                fin(NCH - 3)
                 op2(k, 0, F, nc.vector)
                 x_q(NPAIR - 4, BOTH)
                 op2(k, F, PW, nc.vector)
+                fin(NCH - 3)
             else:
                 if k >= 1:
                     op1(k)
+                if k == 1:
+                    c_q()
                 if k >= 3:
                     x_q(k - 3, BOTH)
                 if k + 2 < NPAIR:

@@ -16,7 +16,6 @@ NCH = 8
 NPAIR = 16
 FLOPS = 2 * B * KIN * F + 2 * B * F * O
 
-N_PLAIN = 6
 GP_SHORT = 704
 GP_LONG = 960
 G_OF_PR = [[0], [0, 1], [0, 1], [1]]
@@ -40,8 +39,6 @@ def tile_chebyshev_l3_sparsed32_stack_pb_t_kernel(tc, z, T3, mask, x1, x2, C_w, 
 
         ident_f = const.tile([P, P], F32, name="ident_f")
         make_identity(nc, ident_f[:])
-        ident_b = const.tile([P, P], BF16, name="ident_b")
-        make_identity(nc, ident_b[:])
 
         z_sb = {}
         x1_sb = {}
@@ -164,25 +161,20 @@ def tile_chebyshev_l3_sparsed32_stack_pb_t_kernel(tc, z, T3, mask, x1, x2, C_w, 
         cc = const.tile([P, 2 * O], U32, name="cc", align_bytes=64)
         cs = const.tile([P, 2 * O], U8, name="cs", align_bytes=64)
 
-        cp = const.tile([P, F], BF16, name="cp")
-
         def bias_spread():
             bt = psum.tile([P, O], F32, name="bt", tag="po", bufs=1)
             nc.tensor.matmul(out=bt[:], lhsT=ones[:], rhs=bias_row[:], start=True, stop=True)
             nc.scalar.copy(out=bias_sb[:], in_=bt[:])
 
-        def c_perm():
-            nc.scalar.copy(
-                out=cp[:].rearrange("p (g t q i) -> p g t q i", g=2, t=4, i=4),
-                in_=c_sb[:].rearrange("p (g q t i) -> p g t q i", g=2, t=4, i=4))
-
         def c_t():
-            ct = psum.tile([P, 8, P], BF16, name="ct", tag="xt", bufs=1)
-            for gt in range(8):
-                nc.tensor.transpose(ct[:, gt, :], cp[:, gt * P:(gt + 1) * P], ident_b[:])
+            cw = c_sb[:].bitcast(F32)
+            ct = psum.tile([P, 4, P], F32, name="ct", tag="xt", bufs=1)
+            for g in range(2):
+                for u in range(2):
+                    nc.tensor.transpose(ct[:, 2 * g + u, :], cw[:, 256 * g + u:256 * (g + 1):2], ident_f[:])
             nc.scalar.copy(
-                out=cg[:].rearrange("p (g o t) -> p g o t", g=2, t=4),
-                in_=ct[:].rearrange("p (g t) o -> p g o t", g=2))
+                out=cg[:].bitcast(F32).rearrange("p (g o u) -> p g o u", g=2, u=2),
+                in_=ct[:].rearrange("p (g u) o -> p g o u", u=2))
 
         def c_q():
             nc.vector.quantize_mx(out=cc[:].bitcast(FP8X4), scales=cs[:], in_=cg[:])
@@ -226,36 +218,34 @@ def tile_chebyshev_l3_sparsed32_stack_pb_t_kernel(tc, z, T3, mask, x1, x2, C_w, 
         def op2(k, lo, hi, eng):
             if k not in x3_sb:
                 x3_sb[k] = work.tile([P, PW], BF16, name="x3_%d" % k, tag="x3", bufs=4)
-            q = slice(lo // 16, hi // 16)
-            x1p = x1_sb[k].rearrange("p (q t i) -> p t q i", t=4, i=4)
-            yp = y_sb[k][:].rearrange("p (q t i) -> p t q i", t=4, i=4)
-            xp = x3_sb[k][:].rearrange("p (t q i) -> p t q i", t=4, i=4)
-            eng.tensor_tensor(out=xp[:, :, q, :], in0=yp[:, :, q, :], in1=x1p[:, :, q, :], op=ALU.subtract)
+            m = slice(lo // 4, hi // 4)
+            x1p = x1_sb[k].rearrange("p (m u e) -> p u m e", u=2, e=2)
+            yp = y_sb[k][:].rearrange("p (m u e) -> p u m e", u=2, e=2)
+            xp = x3_sb[k][:].rearrange("p (u m e) -> p u m e", u=2, e=2)
+            eng.tensor_tensor(out=xp[:, :, m, :], in0=yp[:, :, m, :], in1=x1p[:, :, m, :], op=ALU.subtract)
 
         def x_t(k, unit, tail=False, split=False):
             if unit == 0:
                 xg[k] = work.tile([P, 2 * 1024], BF16, name="xg_%d" % k, tag="xg", bufs=4, align_bytes=64)
-            dst = xg[k][:, unit * 1024:(unit + 1) * 1024].rearrange("p (g b t) -> p g b t", g=2, t=4)
+            dst = xg[k][:].bitcast(F32).rearrange("p (v g b u) -> p v g b u", v=2, g=2, u=2)
+            xw = x3_sb[k][:].bitcast(F32)
             if split:
                 for g in range(2):
-                    xh = psum.tile([P, 4, P], BF16, name="xh", tag="p3", bufs=5)
-                    for t in range(4):
-                        col = t * 512 + unit * 256 + g * P
-                        nc.tensor.transpose(xh[:, t, :], x3_sb[k][:, col:col + P], ident_b[:])
+                    xh = psum.tile([P, 2, P], F32, name="xh", tag="p3", bufs=5)
+                    for u in range(2):
+                        col = u * 512 + unit * 256 + g * P
+                        nc.tensor.transpose(xh[:, u, :], xw[:, col:col + P], ident_f[:])
                     if g == 0:
-                        nc.scalar.copy(out=dst[:, g], in_=xh[:].rearrange("p t b -> p b t"))
+                        nc.scalar.copy(out=dst[:, unit, g], in_=xh[:].rearrange("p u b -> p b u"))
                     else:
-                        nc.vector.tensor_copy(out=dst[:, g], in_=xh[:].rearrange("p t b -> p b t"))
+                        nc.vector.tensor_copy(out=dst[:, unit, g], in_=xh[:].rearrange("p u b -> p b u"))
             else:
-                xt = psum.tile([P, 8, P], BF16, name="xt", tag=("p3" if tail else "xt"), bufs=(5 if tail else 1))
-                for gt in range(8):
-                    col = (gt % 4) * 512 + unit * 256 + (gt // 4) * P
-                    if gt < N_PLAIN:
-                        nc.tensor.matmul(
-                            out=xt[:, gt, :], lhsT=x3_sb[k][:, col:col + P], rhs=ident_b[:], start=True, stop=True)
-                    else:
-                        nc.tensor.transpose(xt[:, gt, :], x3_sb[k][:, col:col + P], ident_b[:])
-                nc.scalar.copy(out=dst, in_=xt[:].rearrange("p (g t) b -> p g b t", g=2))
+                xt = psum.tile([P, 4, P], F32, name="xt", tag=("p3" if tail else "xt"), bufs=(5 if tail else 1))
+                for g in range(2):
+                    for u in range(2):
+                        col = u * 512 + unit * 256 + g * P
+                        nc.tensor.transpose(xt[:, 2 * g + u, :], xw[:, col:col + P], ident_f[:])
+                nc.scalar.copy(out=dst[:, unit], in_=xt[:].rearrange("p (g u) b -> p g b u", u=2))
 
         def x_q(k, units):
             if k not in xc:
@@ -317,12 +307,11 @@ def tile_chebyshev_l3_sparsed32_stack_pb_t_kernel(tc, z, T3, mask, x1, x2, C_w, 
         z_t(2, 1, X_BANK)
         for pr in range(4):
             mm1(0, pr)
-        c_perm()
 
         for k in range(NPAIR):
             last = k == NPAIR - 1
             if k >= 1:
-                nc.gpsimd.tensor_copy(out=mark[:], in_=x3_sb[k - 1][:, 256:257])
+                nc.gpsimd.tensor_copy(out=mark[:], in_=x3_sb[k - 1][:, 512:513])
                 op2(k - 1, 0, gp_cols(k - 1), nc.gpsimd)
             if k in later_loads:
                 cx, cz = later_loads[k]

@@ -18,6 +18,7 @@ FLOPS = 2 * B * KIN * F + 2 * B * F * O
 
 GP_SHORT = 704
 GP_LONG = 960
+WARM = 512
 G_OF_PR = [[0], [0, 1], [0, 1], [1]]
 CI = {(0, 0): 0, (1, 0): 1, (2, 0): 2, (1, 1): 5, (2, 1): 6, (3, 1): 7}
 
@@ -70,10 +71,10 @@ def tile_chebyshev_l3_sparsed32_stack_pb_t_kernel(tc, z, T3, mask, x1, x2, C_w, 
             if fp == 1:
                 load_half(z_sb, zv, 0, 0, "z")
         c_sb = const.tile([P, F], BF16, name="c_sb")
-        bias_row = const.tile([P, O], BF16, name="bias_row")
-        nc.gpsimd.memset(bias_row[:], 0.0)
         ones = const.tile([P, P], BF16, name="ones")
         nc.gpsimd.memset(ones[:], 1.0)
+        bias_row = const.tile([P, O], BF16, name="bias_row")
+        nc.gpsimd.memset(bias_row[:], 0.0)
         bias_sb = const.tile([P, O], F32, name="bias_sb")
         load_half(x2_sb, x2v, 0, 0, "x2")
         load_half(z_sb, zv, 0, 1, "z")
@@ -92,6 +93,10 @@ def tile_chebyshev_l3_sparsed32_stack_pb_t_kernel(tc, z, T3, mask, x1, x2, C_w, 
         load_whole(z_sb, zv, 3, "z")
         later_loads = {1: (2, 4), 2: (3, 5), 3: (4, 6), 4: (5, None), 5: (None, 7), 6: (6, None), 8: (7, None)}
 
+        def busy(bank, times=1):
+            for i in range(times):
+                nc.tensor.matmul(out=bank, lhsT=mk_sb[:, 0:P], rhs=mk_sb[:, 0:WARM], start=True, stop=True)
+
         zg = {}
         zc = {}
         zs = {}
@@ -102,6 +107,8 @@ def tile_chebyshev_l3_sparsed32_stack_pb_t_kernel(tc, z, T3, mask, x1, x2, C_w, 
             zw = z_sb[k].bitcast(F32)
             tag, bufs = early if early else ("tp", 1)
             zt = psum.tile([P, 2, 256], F32, name="zt", tag=tag, bufs=bufs)
+            if g == 1 and k >= 3:
+                busy(zt[:].rearrange("p u c -> p (u c)"))
             for u in range(2):
                 for jl in range(2):
                     col = jl * 512 + 256 * g
@@ -218,33 +225,39 @@ def tile_chebyshev_l3_sparsed32_stack_pb_t_kernel(tc, z, T3, mask, x1, x2, C_w, 
         def op2(k, lo, hi, eng):
             if k not in x3_sb:
                 x3_sb[k] = work.tile([P, PW], BF16, name="x3_%d" % k, tag="x3", bufs=4)
-            m = slice(lo // 4, hi // 4)
-            x1p = x1_sb[k].rearrange("p (m u e) -> p u m e", u=2, e=2)
-            yp = y_sb[k][:].rearrange("p (m u e) -> p u m e", u=2, e=2)
-            xp = x3_sb[k][:].rearrange("p (u m e) -> p u m e", u=2, e=2)
-            eng.tensor_tensor(out=xp[:, :, m, :], in0=yp[:, :, m, :], in1=x1p[:, :, m, :], op=ALU.subtract)
+            x3, y, x1c = x3_sb[k][:, lo:hi], y_sb[k][:, lo:hi], x1_sb[k][:, lo:hi]
+            if lo >= F:
+                x3 = x3.rearrange("p (u m e) -> p u m e", u=2, e=2)
+                y = y.rearrange("p (m u e) -> p u m e", u=2, e=2)
+                x1c = x1c.rearrange("p (m u e) -> p u m e", u=2, e=2)
+            eng.tensor_tensor(out=x3, in0=y, in1=x1c, op=ALU.subtract)
 
-        def x_t(k, unit, tail=False, split=False):
+        def x_words(k, unit, g, u):
+            xw = x3_sb[k][:].bitcast(F32)
+            if unit == 0:
+                return xw[:, 256 * g + u:256 * (g + 1):2]
+            return xw[:, 512 + 256 * u + P * g:512 + 256 * u + P * (g + 1)]
+
+        def x_t(k, unit, bank=("xt", 1), split=False):
             if unit == 0:
                 xg[k] = work.tile([P, 2 * 1024], BF16, name="xg_%d" % k, tag="xg", bufs=4, align_bytes=64)
             dst = xg[k][:].bitcast(F32).rearrange("p (v g b u) -> p v g b u", v=2, g=2, u=2)
-            xw = x3_sb[k][:].bitcast(F32)
             if split:
                 for g in range(2):
                     xh = psum.tile([P, 2, P], F32, name="xh", tag="p3", bufs=5)
                     for u in range(2):
-                        col = u * 512 + unit * 256 + g * P
-                        nc.tensor.transpose(xh[:, u, :], xw[:, col:col + P], ident_f[:])
+                        nc.tensor.transpose(xh[:, u, :], x_words(k, unit, g, u), ident_f[:])
                     if g == 0:
                         nc.scalar.copy(out=dst[:, unit, g], in_=xh[:].rearrange("p u b -> p b u"))
                     else:
                         nc.vector.tensor_copy(out=dst[:, unit, g], in_=xh[:].rearrange("p u b -> p b u"))
             else:
-                xt = psum.tile([P, 4, P], F32, name="xt", tag=("p3" if tail else "xt"), bufs=(5 if tail else 1))
+                xt = psum.tile([P, 4, P], F32, name="xt", tag=bank[0], bufs=bank[1])
+                if unit == 1 or k >= NPAIR - 3:
+                    busy(xt[:].rearrange("p a b -> p (a b)"))
                 for g in range(2):
                     for u in range(2):
-                        col = u * 512 + unit * 256 + g * P
-                        nc.tensor.transpose(xt[:, 2 * g + u, :], xw[:, col:col + P], ident_f[:])
+                        nc.tensor.transpose(xt[:, 2 * g + u, :], x_words(k, unit, g, u), ident_f[:])
                 nc.scalar.copy(out=dst[:, unit], in_=xt[:].rearrange("p (g u) b -> p g b u", u=2))
 
         def x_q(k, units):
@@ -285,33 +298,42 @@ def tile_chebyshev_l3_sparsed32_stack_pb_t_kernel(tc, z, T3, mask, x1, x2, C_w, 
 
         def gp_cols(k):
             return GP_LONG if ((k + 1) % 2 == 0 and k + 1 >= 6) else GP_SHORT
-        P3_BANK, X_BANK = ("p3", 5), ("xt", 1)
+        P3_BANK = ("p3", 5)
+        warm_bank = psum.tile([P, WARM], F32, name="warm_bank", tag="po", bufs=1)
+        busy(warm_bank[:], 5)
         w_mul(0)
         w_mul(1)
         w_t(0, False)
-        z_t(0, 0, P3_BANK)
-        z_t(0, 1, P3_BANK)
+        busy(warm_bank[:], 2)
         w_mul(2)
         w_t(1, False)
+        busy(warm_bank[:])
+        z_t(0, 0, P3_BANK)
+        z_t(0, 1, P3_BANK)
+        busy(warm_bank[:])
         w_mul(3)
         w_q(0)
         w_t(2, False)
+        busy(warm_bank[:], 2)
         z_q(0)
         w_q(1)
         w_t(3, True)
         w_q(2)
+        busy(warm_bank[:], 2)
         z_t(1, 0, P3_BANK)
         w_q(3)
         z_t(1, 1, P3_BANK)
-        z_t(2, 0)
-        z_t(2, 1, X_BANK)
+        busy(warm_bank[:], 2)
         for pr in range(4):
             mm1(0, pr)
+        z_t(2, 0)
+        z_t(2, 1, ("xt", 1))
+        z_q(1)
 
         for k in range(NPAIR):
             last = k == NPAIR - 1
             if k >= 1:
-                nc.gpsimd.tensor_copy(out=mark[:], in_=x3_sb[k - 1][:, 512:513])
+                nc.gpsimd.tensor_copy(out=mark[:], in_=x3_sb[k - 1][:, F:F + 1])
                 op2(k - 1, 0, gp_cols(k - 1), nc.gpsimd)
             if k in later_loads:
                 cx, cz = later_loads[k]
@@ -324,7 +346,6 @@ def tile_chebyshev_l3_sparsed32_stack_pb_t_kernel(tc, z, T3, mask, x1, x2, C_w, 
                 fin((k - 6) // 2)
             if k == 0:
                 op1(0)
-                z_q(1)
             if not last:
                 mm1(k + 1, 0)
                 mm1(k + 1, 1)
@@ -333,7 +354,7 @@ def tile_chebyshev_l3_sparsed32_stack_pb_t_kernel(tc, z, T3, mask, x1, x2, C_w, 
             if k == 0:
                 c_t()
             if k >= 2:
-                x_t(k - 2, 0)
+                x_t(k - 2, 0, ("tp", 1) if last else ("xt", 1))
             if k + 3 < NPAIR:
                 z_t(k + 3, 0)
             if not last:
@@ -354,6 +375,7 @@ def tile_chebyshev_l3_sparsed32_stack_pb_t_kernel(tc, z, T3, mask, x1, x2, C_w, 
                 x_q(NPAIR - 4, BOTH)
                 op2(k, F, PW, nc.vector)
                 fin(NCH - 3)
+                x_q(NPAIR - 3, BOTH)
             else:
                 if k >= 1:
                     op1(k)
@@ -361,24 +383,26 @@ def tile_chebyshev_l3_sparsed32_stack_pb_t_kernel(tc, z, T3, mask, x1, x2, C_w, 
                     c_q()
                 if k >= 3:
                     x_q(k - 3, BOTH)
-                if k + 2 < NPAIR:
+                if k >= 2 and k + 2 < NPAIR:
                     z_q(k + 2)
-                op2(k, gp_cols(k), PW, nc.vector)
+                op2(k, gp_cols(k), F, nc.vector)
+                op2(k, F, PW, nc.vector)
+                if k < 2:
+                    z_q(k + 2)
 
-        x_t(NPAIR - 2, 0, True)
-        x_t(NPAIR - 2, 1, True)
+        x_t(NPAIR - 2, 0, ("tp", 1))
+        x_t(NPAIR - 2, 1)
+        x_t(NPAIR - 1, 0, P3_BANK)
+        x_t(NPAIR - 1, 1, P3_BANK, True)
         mm2(NPAIR - 4, BOTH)
-        x_q(NPAIR - 3, BOTH)
-        x_t(NPAIR - 1, 0, True)
-        mm2(NPAIR - 3, BOTH)
         x_q(NPAIR - 2, BOTH)
-        x_t(NPAIR - 1, 1, True, True)
+        mm2(NPAIR - 3, BOTH)
+        x_q(NPAIR - 1, [0])
         fin(NCH - 2)
         mm2(NPAIR - 2, BOTH)
-        x_q(NPAIR - 1, [0])
         mm2(NPAIR - 1, [0])
-        fin(NCH - 1, (NPAIR - 2, 0), 0, 2)
         x_q(NPAIR - 1, [1])
         mm2(NPAIR - 1, [1])
+        fin(NCH - 1, (NPAIR - 2, 0), 0, 2)
         fin(NCH - 1, (NPAIR - 1, 0), 2, 1)
         fin(NCH - 1, (NPAIR - 1, 1), 3, 1)

@@ -107,8 +107,6 @@ def tile_chebyshev_l3_sparsed32_stack_pb_t_kernel(tc, z, T3, mask, x1, x2, C_w, 
             zw = z_sb[k].bitcast(F32)
             tag, bufs = early if early else ("tp", 1)
             zt = psum.tile([P, 2, 256], F32, name="zt", tag=tag, bufs=bufs)
-            if g == 1 and k >= 3:
-                busy(zt[:].rearrange("p u c -> p (u c)"))
             for u in range(2):
                 for jl in range(2):
                     col = jl * 512 + 256 * g
@@ -225,18 +223,13 @@ def tile_chebyshev_l3_sparsed32_stack_pb_t_kernel(tc, z, T3, mask, x1, x2, C_w, 
         def op2(k, lo, hi, eng):
             if k not in x3_sb:
                 x3_sb[k] = work.tile([P, PW], BF16, name="x3_%d" % k, tag="x3", bufs=4)
-            x3, y, x1c = x3_sb[k][:, lo:hi], y_sb[k][:, lo:hi], x1_sb[k][:, lo:hi]
-            if lo >= F:
-                x3 = x3.rearrange("p (u m e) -> p u m e", u=2, e=2)
-                y = y.rearrange("p (m u e) -> p u m e", u=2, e=2)
-                x1c = x1c.rearrange("p (m u e) -> p u m e", u=2, e=2)
-            eng.tensor_tensor(out=x3, in0=y, in1=x1c, op=ALU.subtract)
+            cols = slice(lo, hi)
+            eng.tensor_tensor(out=x3_sb[k][:, cols], in0=y_sb[k][:, cols], in1=x1_sb[k][:, cols], op=ALU.subtract)
 
         def x_words(k, unit, g, u):
             xw = x3_sb[k][:].bitcast(F32)
-            if unit == 0:
-                return xw[:, 256 * g + u:256 * (g + 1):2]
-            return xw[:, 512 + 256 * u + P * g:512 + 256 * u + P * (g + 1)]
+            first = unit * 512 + 256 * g
+            return xw[:, first + u:first + 256:2]
 
         def x_t(k, unit, bank=("xt", 1), split=False):
             if unit == 0:
@@ -385,8 +378,7 @@ def tile_chebyshev_l3_sparsed32_stack_pb_t_kernel(tc, z, T3, mask, x1, x2, C_w, 
                     x_q(k - 3, BOTH)
                 if k >= 2 and k + 2 < NPAIR:
                     z_q(k + 2)
-                op2(k, gp_cols(k), F, nc.vector)
-                op2(k, F, PW, nc.vector)
+                op2(k, gp_cols(k), PW, nc.vector)
                 if k < 2:
                     z_q(k + 2)
 

@@ -68,8 +68,7 @@ def tile_chebyshev_l3_sparsed32_stack_pb_t_kernel(tc, z, T3, mask, x1, x2, C_w, 
             nc.sync.dma_start(
                 out=t3h[hh][:, lo:lo + 2 * KIN].rearrange("p (f k) -> p f k", f=2),
                 in_=t3v[:, 2 * fp:2 * fp + 2, :])
-            if fp == 1:
-                load_half(z_sb, zv, 0, 0, "z")
+        load_half(z_sb, zv, 0, 0, "z")
         c_sb = const.tile([P, F], BF16, name="c_sb")
         ones = const.tile([P, P], BF16, name="ones")
         nc.gpsimd.memset(ones[:], 1.0)
@@ -98,21 +97,28 @@ def tile_chebyshev_l3_sparsed32_stack_pb_t_kernel(tc, z, T3, mask, x1, x2, C_w, 
                 nc.tensor.matmul(out=bank, lhsT=mk_sb[:, 0:P], rhs=mk_sb[:, 0:WARM], start=True, stop=True)
 
         zg = {}
+        zp = {}
         zc = {}
         zs = {}
 
         def z_t(k, g, early=None):
             if g == 0:
                 zg[k] = work.tile([P, 2 * 256 * 4], BF16, name="zg_%d" % k, tag="zg", align_bytes=64)
-            zw = z_sb[k].bitcast(F32)
+            zw = zp[k][:] if k in zp else z_sb[k].bitcast(F32)
             tag, bufs = early if early else ("tp", 1)
             zt = psum.tile([P, 2, 256], F32, name="zt", tag=tag, bufs=bufs)
             for u in range(2):
                 for jl in range(2):
                     col = jl * 512 + 256 * g
-                    nc.tensor.transpose(zt[:, u, jl * P:(jl + 1) * P], zw[:, col + u:col + 256:2], ident_f[:])
+                    words = zw[:, col + u * P:col + (u + 1) * P] if k in zp else zw[:, col + u:col + 256:2]
+                    nc.tensor.transpose(zt[:, u, jl * P:(jl + 1) * P], words, ident_f[:])
             zgw = zg[k][:].bitcast(F32).rearrange("p (g c u) -> p g c u", g=2, u=2)
             nc.scalar.copy(out=zgw[:, g, :, :], in_=zt[:].rearrange("p u c -> p c u"))
+
+        def z_perm(k):
+            zp[k] = work.tile([P, KIN], F32, name="zp_%d" % k, tag="zp", bufs=2)
+            nc.scalar.copy(out=zp[k][:].rearrange("p (a u w) -> p a u w", u=2, w=P),
+                           in_=z_sb[k].bitcast(F32).rearrange("p (a w u) -> p a u w", u=2, w=P))
 
         def z_q(k):
             zc[k] = work.tile([P, 512], U32, name="zc_%d" % k, tag="zc", bufs=4, align_bytes=64)
@@ -287,6 +293,7 @@ def tile_chebyshev_l3_sparsed32_stack_pb_t_kernel(tc, z, T3, mask, x1, x2, C_w, 
                               in_=o_sb[:, lo:lo + n, :].rearrange("p j o -> p (j o)"))
 
         mark = const.tile([P, 1], BF16, name="mark")
+        mark_u = const.tile([P, 1], U32, name="mark_u")
         BOTH = [0, 1]
 
         def gp_cols(k):
@@ -300,21 +307,21 @@ def tile_chebyshev_l3_sparsed32_stack_pb_t_kernel(tc, z, T3, mask, x1, x2, C_w, 
         busy(warm_bank[:], 2)
         w_mul(2)
         w_t(1, False)
-        busy(warm_bank[:])
+        busy(warm_bank[:], 2)
+        w_mul(3)
+        w_t(2, True)
+        busy(warm_bank[:], 2)
+        w_q(0)
+        w_t(3, True)
+        busy(warm_bank[:], 2)
+        w_q(1)
         z_t(0, 0, P3_BANK)
         z_t(0, 1, P3_BANK)
-        busy(warm_bank[:])
-        w_mul(3)
-        w_q(0)
-        w_t(2, False)
         busy(warm_bank[:], 2)
-        z_q(0)
-        w_q(1)
-        w_t(3, True)
         w_q(2)
-        busy(warm_bank[:], 2)
-        z_t(1, 0, P3_BANK)
         w_q(3)
+        z_q(0)
+        z_t(1, 0, P3_BANK)
         z_t(1, 1, P3_BANK)
         busy(warm_bank[:], 2)
         for pr in range(4):
@@ -326,7 +333,11 @@ def tile_chebyshev_l3_sparsed32_stack_pb_t_kernel(tc, z, T3, mask, x1, x2, C_w, 
         for k in range(NPAIR):
             last = k == NPAIR - 1
             if k >= 1:
-                nc.gpsimd.tensor_copy(out=mark[:], in_=x3_sb[k - 1][:, F:F + 1])
+                if k - 1 < 2:
+                    nc.gpsimd.tensor_copy(out=mark[:], in_=x3_sb[k - 1][:, PW - 1:PW])
+                else:
+                    codes = zc[k + 1] if k + 1 < NPAIR else xc[k - 4]
+                    nc.gpsimd.tensor_copy(out=mark_u[:], in_=codes[:, 511:512])
                 op2(k - 1, 0, gp_cols(k - 1), nc.gpsimd)
             if k in later_loads:
                 cx, cz = later_loads[k]
@@ -335,8 +346,6 @@ def tile_chebyshev_l3_sparsed32_stack_pb_t_kernel(tc, z, T3, mask, x1, x2, C_w, 
                     load_whole(x1_sb, x1v, cx, "x1")
                 if cz is not None:
                     load_whole(z_sb, zv, cz, "z")
-            if k >= 6 and k % 2 == 0:
-                fin((k - 6) // 2)
             if k == 0:
                 op1(0)
             if not last:
@@ -350,6 +359,8 @@ def tile_chebyshev_l3_sparsed32_stack_pb_t_kernel(tc, z, T3, mask, x1, x2, C_w, 
                 x_t(k - 2, 0, ("tp", 1) if last else ("xt", 1))
             if k + 3 < NPAIR:
                 z_t(k + 3, 0)
+            if k + 4 < NPAIR:
+                z_perm(k + 4)
             if not last:
                 mm1(k + 1, 2)
                 mm1(k + 1, 3)
@@ -372,6 +383,8 @@ def tile_chebyshev_l3_sparsed32_stack_pb_t_kernel(tc, z, T3, mask, x1, x2, C_w, 
             else:
                 if k >= 1:
                     op1(k)
+                if k >= 6 and k % 2 == 0:
+                    fin((k - 6) // 2)
                 if k == 1:
                     c_q()
                 if k >= 3:

@@ -16,8 +16,8 @@ NCH = 8
 NPAIR = 16
 FLOPS = 2 * B * KIN * F + 2 * B * F * O
 
-GP_SHORT = 704
-GP_LONG = 960
+GP_COLS = 1024
+PS_COLS = 512
 WARM = 512
 G_OF_PR = [[0], [0, 1], [0, 1], [1]]
 CI = {(0, 0): 0, (1, 0): 1, (2, 0): 2, (1, 1): 5, (2, 1): 6, (3, 1): 7}
@@ -41,6 +41,8 @@ def tile_chebyshev_l3_sparsed32_stack_pb_t_kernel(tc, z, T3, mask, x1, x2, C_w, 
         ident_f = const.tile([P, P], F32, name="ident_f")
         make_identity(nc, ident_f[:])
 
+        ident_b = const.tile([P, P], BF16, name="ident_b")
+        make_identity(nc, ident_b[:])
         z_sb = {}
         x1_sb = {}
         x2_sb = {}
@@ -148,7 +150,7 @@ def tile_chebyshev_l3_sparsed32_stack_pb_t_kernel(tc, z, T3, mask, x1, x2, C_w, 
             hh, lo = fp // 2, (fp % 2) * 2 * KIN
             ww = wm[hh][:]
             for g in range(2):
-                wt = psum.tile([P, 2, 256], F32, name="wt", tag="p3", bufs=5)
+                wt = psum.tile([P, 2, 256], F32, name="wt", tag="p3", bufs=4)
                 for u in range(2):
                     for fl in range(2):
                         col = lo // 2 + u * 512 + fl * 256 + g * P
@@ -199,7 +201,7 @@ def tile_chebyshev_l3_sparsed32_stack_pb_t_kernel(tc, z, T3, mask, x1, x2, C_w, 
         po = {}
 
         def mm1(k, pr):
-            bank = psum.tile([P, 512], F32, name="p3_%d_%d" % (k, pr), tag="p3", bufs=5)
+            bank = psum.tile([P, 512], F32, name="p3_%d_%d" % (k, pr), tag="p3", bufs=4)
             p3[(k, pr)] = bank
             gs = G_OF_PR[pr]
             for jl in range(2):
@@ -232,6 +234,17 @@ def tile_chebyshev_l3_sparsed32_stack_pb_t_kernel(tc, z, T3, mask, x1, x2, C_w, 
             cols = slice(lo, hi)
             eng.tensor_tensor(out=x3_sb[k][:, cols], in0=y_sb[k][:, cols], in1=x1_sb[k][:, cols], op=ALU.subtract)
 
+        xb = {}
+
+        def x1_bank(k):
+            xb[k] = psum.tile([P, PS_COLS], F32, name="xb", tag="xb", bufs=1)
+            nc.tensor.matmul(out=xb[k][:], lhsT=ident_b[:], rhs=x1_sb[k][:, GP_COLS:GP_COLS + PS_COLS],
+                             start=True, stop=True)
+
+        def op2_bank(k):
+            cols = slice(GP_COLS, GP_COLS + PS_COLS)
+            nc.vector.tensor_tensor(out=x3_sb[k][:, cols], in0=y_sb[k][:, cols], in1=xb[k][:], op=ALU.subtract)
+
         def x_words(k, unit, g, u):
             xw = x3_sb[k][:].bitcast(F32)
             first = unit * 512 + 256 * g
@@ -243,7 +256,7 @@ def tile_chebyshev_l3_sparsed32_stack_pb_t_kernel(tc, z, T3, mask, x1, x2, C_w, 
             dst = xg[k][:].bitcast(F32).rearrange("p (v g b u) -> p v g b u", v=2, g=2, u=2)
             if split:
                 for g in range(2):
-                    xh = psum.tile([P, 2, P], F32, name="xh", tag="p3", bufs=5)
+                    xh = psum.tile([P, 2, P], F32, name="xh", tag="p3", bufs=4)
                     for u in range(2):
                         nc.tensor.transpose(xh[:, u, :], x_words(k, unit, g, u), ident_f[:])
                     if g == 0:
@@ -252,8 +265,6 @@ def tile_chebyshev_l3_sparsed32_stack_pb_t_kernel(tc, z, T3, mask, x1, x2, C_w, 
                         nc.vector.tensor_copy(out=dst[:, unit, g], in_=xh[:].rearrange("p u b -> p b u"))
             else:
                 xt = psum.tile([P, 4, P], F32, name="xt", tag=bank[0], bufs=bank[1])
-                if unit == 1 or k >= NPAIR - 3:
-                    busy(xt[:].rearrange("p a b -> p (a b)"))
                 for g in range(2):
                     for u in range(2):
                         nc.tensor.transpose(xt[:, 2 * g + u, :], x_words(k, unit, g, u), ident_f[:])
@@ -272,7 +283,7 @@ def tile_chebyshev_l3_sparsed32_stack_pb_t_kernel(tc, z, T3, mask, x1, x2, C_w, 
             key = c if c < NCH - 1 else (k, units[0])
             if key not in po:
                 po[key] = psum.tile([P, 4, O], F32, name="po_%d" % c,
-                                    tag=("po" if c < NCH - 1 else "p3"), bufs=(1 if c < NCH - 1 else 5))
+                                    tag=("po" if c < NCH - 1 else "p3"), bufs=(1 if c < NCH - 1 else 4))
             for unit in units:
                 for g in range(2):
                     lo = (unit * 2 + g) * P
@@ -296,34 +307,26 @@ def tile_chebyshev_l3_sparsed32_stack_pb_t_kernel(tc, z, T3, mask, x1, x2, C_w, 
         mark_u = const.tile([P, 1], U32, name="mark_u")
         BOTH = [0, 1]
 
-        def gp_cols(k):
-            return GP_LONG if ((k + 1) % 2 == 0 and k + 1 >= 6) else GP_SHORT
-        P3_BANK = ("p3", 5)
+        P3_BANK = ("p3", 4)
         warm_bank = psum.tile([P, WARM], F32, name="warm_bank", tag="po", bufs=1)
-        busy(warm_bank[:], 5)
+        busy(warm_bank[:], 6)
         w_mul(0)
         w_mul(1)
         w_t(0, False)
-        busy(warm_bank[:], 2)
         w_mul(2)
         w_t(1, False)
-        busy(warm_bank[:], 2)
         w_mul(3)
         w_t(2, True)
-        busy(warm_bank[:], 2)
         w_q(0)
         w_t(3, True)
-        busy(warm_bank[:], 2)
         w_q(1)
         z_t(0, 0, P3_BANK)
         z_t(0, 1, P3_BANK)
-        busy(warm_bank[:], 2)
         w_q(2)
         w_q(3)
         z_q(0)
         z_t(1, 0, P3_BANK)
         z_t(1, 1, P3_BANK)
-        busy(warm_bank[:], 2)
         for pr in range(4):
             mm1(0, pr)
         z_t(2, 0)
@@ -338,7 +341,7 @@ def tile_chebyshev_l3_sparsed32_stack_pb_t_kernel(tc, z, T3, mask, x1, x2, C_w, 
                 else:
                     codes = zc[k + 1] if k + 1 < NPAIR else xc[k - 4]
                     nc.gpsimd.tensor_copy(out=mark_u[:], in_=codes[:, 511:512])
-                op2(k - 1, 0, gp_cols(k - 1), nc.gpsimd)
+                op2(k - 1, 0, GP_COLS, nc.gpsimd)
             if k in later_loads:
                 cx, cz = later_loads[k]
                 if cx is not None:
@@ -348,6 +351,8 @@ def tile_chebyshev_l3_sparsed32_stack_pb_t_kernel(tc, z, T3, mask, x1, x2, C_w, 
                     load_whole(z_sb, zv, cz, "z")
             if k == 0:
                 op1(0)
+            if k >= 1:
+                x1_bank(k - 1)
             if not last:
                 mm1(k + 1, 0)
                 mm1(k + 1, 1)
@@ -375,6 +380,7 @@ def tile_chebyshev_l3_sparsed32_stack_pb_t_kernel(tc, z, T3, mask, x1, x2, C_w, 
             if last:
                 op1(k, [0])
                 op1(k, [1])
+                op2_bank(k - 1)
                 op2(k, 0, F, nc.vector)
                 x_q(NPAIR - 4, BOTH)
                 op2(k, F, PW, nc.vector)
@@ -383,6 +389,8 @@ def tile_chebyshev_l3_sparsed32_stack_pb_t_kernel(tc, z, T3, mask, x1, x2, C_w, 
             else:
                 if k >= 1:
                     op1(k)
+                if k >= 1:
+                    op2_bank(k - 1)
                 if k >= 6 and k % 2 == 0:
                     fin((k - 6) // 2)
                 if k == 1:
@@ -391,7 +399,7 @@ def tile_chebyshev_l3_sparsed32_stack_pb_t_kernel(tc, z, T3, mask, x1, x2, C_w, 
                     x_q(k - 3, BOTH)
                 if k >= 2 and k + 2 < NPAIR:
                     z_q(k + 2)
-                op2(k, gp_cols(k), PW, nc.vector)
+                op2(k, GP_COLS + PS_COLS, PW, nc.vector)
                 if k < 2:
                     z_q(k + 2)
 

@@ -16,7 +16,7 @@ NCH = 8
 NPAIR = 16
 FLOPS = 2 * B * KIN * F + 2 * B * F * O
 
-GP_COLS = 1024
+GP_COLS = 1088
 PS_COLS = 512
 WARM = 512
 G_OF_PR = [[0], [0, 1], [0, 1], [1]]
@@ -53,6 +53,15 @@ def tile_chebyshev_l3_sparsed32_stack_pb_t_kernel(tc, z, T3, mask, x1, x2, C_w, 
             nc.sync.dma_start(out=t[:], in_=src[c][:, hf * PW:(hf + 1) * PW])
             dst[2 * c + hf] = t[:]
 
+        parts = {}
+
+        def load_part(dst, src, c, hf, tag):
+            if (tag, c) not in parts:
+                parts[(tag, c)] = stream.tile([P, 2 * PW], BF16, name="%s_%d" % (tag, c), tag=tag)
+            t = parts[(tag, c)]
+            nc.sync.dma_start(out=t[:, hf * PW:(hf + 1) * PW], in_=src[c][:, hf * PW:(hf + 1) * PW])
+            dst[2 * c + hf] = t[:, hf * PW:(hf + 1) * PW]
+
         def load_whole(dst, src, c, tag):
             t = stream.tile([P, 2 * PW], BF16, name="%s_%d" % (tag, c), tag=tag)
             nc.sync.dma_start(out=t[:], in_=src[c])
@@ -80,18 +89,20 @@ def tile_chebyshev_l3_sparsed32_stack_pb_t_kernel(tc, z, T3, mask, x1, x2, C_w, 
         load_half(x2_sb, x2v, 0, 0, "x2")
         load_half(z_sb, zv, 0, 1, "z")
         load_half(z_sb, zv, 1, 0, "z")
-        nc.sync.dma_start(out=c_sb[:], in_=C_w)
         load_half(x1_sb, x1v, 0, 0, "x1")
-        nc.sync.dma_start(out=bias_row[0:1, :], in_=C_b.unsqueeze(0))
-        load_half(x2_sb, x2v, 0, 1, "x2")
-        load_half(x1_sb, x1v, 0, 1, "x1")
         load_half(z_sb, zv, 1, 1, "z")
+        load_half(x2_sb, x2v, 0, 1, "x2")
+        load_part(z_sb, zv, 2, 0, "z")
+        load_half(x1_sb, x1v, 0, 1, "x1")
+        nc.sync.dma_start(out=c_sb[:], in_=C_w)
+        nc.sync.dma_start(out=bias_row[0:1, :], in_=C_b.unsqueeze(0))
         load_half(x2_sb, x2v, 1, 0, "x2")
+        load_part(z_sb, zv, 2, 1, "z")
         load_half(x1_sb, x1v, 1, 0, "x1")
-        load_whole(z_sb, zv, 2, "z")
         load_half(x2_sb, x2v, 1, 1, "x2")
+        load_part(z_sb, zv, 3, 0, "z")
         load_half(x1_sb, x1v, 1, 1, "x1")
-        load_whole(z_sb, zv, 3, "z")
+        load_part(z_sb, zv, 3, 1, "z")
         later_loads = {1: (2, 4), 2: (3, 5), 3: (4, 6), 4: (5, None), 5: (None, 7), 6: (6, None), 8: (7, None)}
 
         def busy(bank, times=1):
@@ -137,7 +148,7 @@ def tile_chebyshev_l3_sparsed32_stack_pb_t_kernel(tc, z, T3, mask, x1, x2, C_w, 
         def w_mul(fp):
             hh, lo = fp // 2, (fp % 2) * 2 * KIN
             if fp % 2 == 0:
-                wm_t = work.tile([P, PW], F32, name="wm_%d" % hh, tag="y")
+                wm_t = work.tile([P, PW], F32, name="wm_%d" % hh, tag="y", bufs=2)
                 wm.append(wm_t)
             dst = wm[hh][:].bitcast(BF16)[:, lo:lo + 2 * KIN]
             nc.vector.tensor_tensor(
@@ -216,7 +227,7 @@ def tile_chebyshev_l3_sparsed32_stack_pb_t_kernel(tc, z, T3, mask, x1, x2, C_w, 
 
         def op1(k, units=(0, 1)):
             if k not in y_sb:
-                y_sb[k] = work.tile([P, PW], F32, name="y_%d" % k, tag="y")
+                y_sb[k] = work.tile([P, PW], F32, name="y_%d" % k, tag="y", bufs=2)
             ss = slice(16 * units[0], 16 * units[-1] + 16)
             yv = y_sb[k][:].rearrange("p (s q) -> p s q", q=64)
             x2u = x2_sb[k].rearrange("p (s q) -> p s q", q=64)
@@ -230,7 +241,7 @@ def tile_chebyshev_l3_sparsed32_stack_pb_t_kernel(tc, z, T3, mask, x1, x2, C_w, 
 
         def op2(k, lo, hi, eng):
             if k not in x3_sb:
-                x3_sb[k] = work.tile([P, PW], BF16, name="x3_%d" % k, tag="x3", bufs=4)
+                x3_sb[k] = work.tile([P, PW], BF16, name="x3_%d" % k, tag="x3", bufs=3)
             cols = slice(lo, hi)
             eng.tensor_tensor(out=x3_sb[k][:, cols], in0=y_sb[k][:, cols], in1=x1_sb[k][:, cols], op=ALU.subtract)
 
@@ -245,6 +256,12 @@ def tile_chebyshev_l3_sparsed32_stack_pb_t_kernel(tc, z, T3, mask, x1, x2, C_w, 
             cols = slice(GP_COLS, GP_COLS + PS_COLS)
             nc.vector.tensor_tensor(out=x3_sb[k][:, cols], in0=y_sb[k][:, cols], in1=xb[k][:], op=ALU.subtract)
 
+        def op2_end(k, i):
+            cols = slice(512 * i, 512 * i + 512)
+            xe = psum.tile([P, 512], F32, name="xe_%d" % i, tag="p3", bufs=4)
+            nc.tensor.matmul(out=xe[:], lhsT=ident_b[:], rhs=x1_sb[k][:, cols], start=True, stop=True)
+            nc.vector.tensor_tensor(out=x3_sb[k][:, cols], in0=y_sb[k][:, cols], in1=xe[:], op=ALU.subtract)
+
         def x_words(k, unit, g, u):
             xw = x3_sb[k][:].bitcast(F32)
             first = unit * 512 + 256 * g
@@ -252,7 +269,7 @@ def tile_chebyshev_l3_sparsed32_stack_pb_t_kernel(tc, z, T3, mask, x1, x2, C_w, 
 
         def x_t(k, unit, bank=("xt", 1), split=False):
             if unit == 0:
-                xg[k] = work.tile([P, 2 * 1024], BF16, name="xg_%d" % k, tag="xg", bufs=4, align_bytes=64)
+                xg[k] = work.tile([P, 2 * 1024], BF16, name="xg_%d" % k, tag="xg", bufs=3, align_bytes=64)
             dst = xg[k][:].bitcast(F32).rearrange("p (v g b u) -> p v g b u", v=2, g=2, u=2)
             if split:
                 for g in range(2):
@@ -296,7 +313,7 @@ def tile_chebyshev_l3_sparsed32_stack_pb_t_kernel(tc, z, T3, mask, x1, x2, C_w, 
         o_last = const.tile([P, 4, O], F32, name="o_last")
 
         def fin(c, key=None, lo=0, n=4):
-            o_sb = o_last if key else work.tile([P, 4, O], F32, name="o_sb", tag="o_sb", bufs=2)
+            o_sb = o_last if key else work.tile([P, 4, O], F32, name="o_sb", tag="o_sb", bufs=7)
             nc.vector.tensor_tensor(
                 out=o_sb[:, lo:lo + n, :], in0=po[c if key is None else key][:, lo:lo + n, :],
                 in1=bias_sb[:].unsqueeze(1).to_broadcast([P, n, O]), op=ALU.add)
@@ -344,11 +361,12 @@ def tile_chebyshev_l3_sparsed32_stack_pb_t_kernel(tc, z, T3, mask, x1, x2, C_w, 
                 op2(k - 1, 0, GP_COLS, nc.gpsimd)
             if k in later_loads:
                 cx, cz = later_loads[k]
-                if cx is not None:
-                    load_whole(x2_sb, x2v, cx, "x2")
-                    load_whole(x1_sb, x1v, cx, "x1")
-                if cz is not None:
-                    load_whole(z_sb, zv, cz, "z")
+                for hf in range(2):
+                    if cx is not None:
+                        load_part(x2_sb, x2v, cx, hf, "x2")
+                        load_part(x1_sb, x1v, cx, hf, "x1")
+                    if cz is not None:
+                        load_part(z_sb, zv, cz, hf, "z")
             if k == 0:
                 op1(0)
             if k >= 1:
@@ -358,7 +376,7 @@ def tile_chebyshev_l3_sparsed32_stack_pb_t_kernel(tc, z, T3, mask, x1, x2, C_w, 
                 mm1(k + 1, 1)
             if last:
                 mm2(k - 4, BOTH)
-            if k == 0:
+            if k == 1:
                 c_t()
             if k >= 2:
                 x_t(k - 2, 0, ("tp", 1) if last else ("xt", 1))
@@ -371,7 +389,7 @@ def tile_chebyshev_l3_sparsed32_stack_pb_t_kernel(tc, z, T3, mask, x1, x2, C_w, 
                 mm1(k + 1, 3)
             if 4 <= k and not last:
                 mm2(k - 4, BOTH)
-            if k == 2:
+            if k == 3:
                 bias_spread()
             if k >= 2:
                 x_t(k - 2, 1)
@@ -380,10 +398,11 @@ def tile_chebyshev_l3_sparsed32_stack_pb_t_kernel(tc, z, T3, mask, x1, x2, C_w, 
             if last:
                 op1(k, [0])
                 op1(k, [1])
+                op2(k, 0, 512, nc.gpsimd)
                 op2_bank(k - 1)
-                op2(k, 0, F, nc.vector)
+                for i in range(1, 4):
+                    op2_end(k, i)
                 x_q(NPAIR - 4, BOTH)
-                op2(k, F, PW, nc.vector)
                 fin(NCH - 3)
                 x_q(NPAIR - 3, BOTH)
             else:
@@ -393,7 +412,7 @@ def tile_chebyshev_l3_sparsed32_stack_pb_t_kernel(tc, z, T3, mask, x1, x2, C_w, 
                     op2_bank(k - 1)
                 if k >= 6 and k % 2 == 0:
                     fin((k - 6) // 2)
-                if k == 1:
+                if k == 2:
                     c_q()
                 if k >= 3:
                     x_q(k - 3, BOTH)

@@ -16,8 +16,8 @@ NCH = 8
 NPAIR = 16
 FLOPS = 2 * B * KIN * F + 2 * B * F * O
 
-GP_COLS = 1088
-PS_COLS = 512
+GP_GROUPS = 17
+PS_GROUPS = 8
 WARM = 512
 G_OF_PR = [[0], [0, 1], [0, 1], [1]]
 CI = {(0, 0): 0, (1, 0): 1, (2, 0): 2, (1, 1): 5, (2, 1): 6, (3, 1): 7}
@@ -191,11 +191,13 @@ def tile_chebyshev_l3_sparsed32_stack_pb_t_kernel(tc, z, T3, mask, x1, x2, C_w, 
             nc.scalar.copy(out=bias_sb[:], in_=bt[:])
 
         def c_t():
-            cw = c_sb[:].bitcast(F32)
+            cw = const.tile([P, F // 2], F32, name="cw")
+            nc.scalar.copy(out=cw[:].rearrange("p (pr s w) -> p pr s w", pr=4, w=8),
+                           in_=c_sb[:].bitcast(F32).rearrange("p (s pr w) -> p pr s w", pr=4, w=8))
             ct = psum.tile([P, 4, P], F32, name="ct", tag="xt", bufs=1)
             for g in range(2):
                 for u in range(2):
-                    nc.tensor.transpose(ct[:, 2 * g + u, :], cw[:, 256 * g + u:256 * (g + 1):2], ident_f[:])
+                    nc.tensor.transpose(ct[:, 2 * g + u, :], cw[:, (2 * g + u) * P:(2 * g + u + 1) * P], ident_f[:])
             nc.scalar.copy(
                 out=cg[:].bitcast(F32).rearrange("p (g o u) -> p g o u", g=2, u=2),
                 in_=ct[:].rearrange("p (g u) o -> p g o u", u=2))
@@ -229,43 +231,48 @@ def tile_chebyshev_l3_sparsed32_stack_pb_t_kernel(tc, z, T3, mask, x1, x2, C_w, 
             if k not in y_sb:
                 y_sb[k] = work.tile([P, PW], F32, name="y_%d" % k, tag="y", bufs=2)
             ss = slice(16 * units[0], 16 * units[-1] + 16)
-            yv = y_sb[k][:].rearrange("p (s q) -> p s q", q=64)
+            yv = y_sb[k][:].rearrange("p (pr s r) -> p pr s r", pr=4, r=16)
             x2u = x2_sb[k].rearrange("p (s q) -> p s q", q=64)
             for pr in range(4):
                 nc.vector.scalar_tensor_tensor(
-                    out=yv[:, ss, pr * 16:(pr + 1) * 16],
+                    out=yv[:, pr, ss, :],
                     in0=p3[(k, pr)][:].rearrange("p (s r) -> p s r", r=16)[:, ss, :],
                     scalar=2.0,
                     in1=x2u[:, ss, pr * 16:(pr + 1) * 16],
                     op0=ALU.mult, op1=ALU.mult)
 
-        def op2(k, lo, hi, eng):
+        def by_pr(view):
+            return view.rearrange("p (s pr r) -> p pr s r", pr=4, r=16)
+
+        def subtract(k, lo, hi, x1_view, eng):
             if k not in x3_sb:
                 x3_sb[k] = work.tile([P, PW], BF16, name="x3_%d" % k, tag="x3", bufs=3)
-            cols = slice(lo, hi)
-            eng.tensor_tensor(out=x3_sb[k][:, cols], in0=y_sb[k][:, cols], in1=x1_sb[k][:, cols], op=ALU.subtract)
+            yv = y_sb[k][:].rearrange("p (pr s r) -> p pr s r", pr=4, r=16)
+            xv = x3_sb[k][:].rearrange("p (pr s r) -> p pr s r", pr=4, r=16)
+            eng.tensor_tensor(out=xv[:, :, lo:hi, :], in0=yv[:, :, lo:hi, :], in1=by_pr(x1_view), op=ALU.subtract)
+
+        def op2(k, lo, hi, eng):
+            subtract(k, lo, hi, x1_sb[k][:, 64 * lo:64 * hi], eng)
 
         xb = {}
 
         def x1_bank(k):
-            xb[k] = psum.tile([P, PS_COLS], F32, name="xb", tag="xb", bufs=1)
-            nc.tensor.matmul(out=xb[k][:], lhsT=ident_b[:], rhs=x1_sb[k][:, GP_COLS:GP_COLS + PS_COLS],
+            xb[k] = psum.tile([P, 64 * PS_GROUPS], F32, name="xb", tag="xb", bufs=1)
+            nc.tensor.matmul(out=xb[k][:], lhsT=ident_b[:], rhs=x1_sb[k][:, 64 * GP_GROUPS:64 * (GP_GROUPS + PS_GROUPS)],
                              start=True, stop=True)
 
         def op2_bank(k):
-            cols = slice(GP_COLS, GP_COLS + PS_COLS)
-            nc.vector.tensor_tensor(out=x3_sb[k][:, cols], in0=y_sb[k][:, cols], in1=xb[k][:], op=ALU.subtract)
+            subtract(k, GP_GROUPS, GP_GROUPS + PS_GROUPS, xb[k][:], nc.vector)
 
         def op2_end(k, i):
             cols = slice(512 * i, 512 * i + 512)
             xe = psum.tile([P, 512], F32, name="xe_%d" % i, tag="p3", bufs=4)
             nc.tensor.matmul(out=xe[:], lhsT=ident_b[:], rhs=x1_sb[k][:, cols], start=True, stop=True)
-            nc.vector.tensor_tensor(out=x3_sb[k][:, cols], in0=y_sb[k][:, cols], in1=xe[:], op=ALU.subtract)
+            subtract(k, 8 * i, 8 * i + 8, xe[:], nc.vector)
 
         def x_words(k, unit, g, u):
-            xw = x3_sb[k][:].bitcast(F32)
-            first = unit * 512 + 256 * g
-            return xw[:, first + u:first + 256:2]
+            first = (2 * g + u) * 256 + unit * P
+            return x3_sb[k][:].bitcast(F32)[:, first:first + P]
 
         def x_t(k, unit, bank=("xt", 1), split=False):
             if unit == 0:
@@ -358,7 +365,7 @@ def tile_chebyshev_l3_sparsed32_stack_pb_t_kernel(tc, z, T3, mask, x1, x2, C_w, 
                 else:
                     codes = zc[k + 1] if k + 1 < NPAIR else xc[k - 4]
                     nc.gpsimd.tensor_copy(out=mark_u[:], in_=codes[:, 511:512])
-                op2(k - 1, 0, GP_COLS, nc.gpsimd)
+                op2(k - 1, 0, GP_GROUPS, nc.gpsimd)
             if k in later_loads:
                 cx, cz = later_loads[k]
                 for hf in range(2):
@@ -398,7 +405,7 @@ def tile_chebyshev_l3_sparsed32_stack_pb_t_kernel(tc, z, T3, mask, x1, x2, C_w, 
             if last:
                 op1(k, [0])
                 op1(k, [1])
-                op2(k, 0, 512, nc.gpsimd)
+                op2(k, 0, 8, nc.gpsimd)
                 op2_bank(k - 1)
                 for i in range(1, 4):
                     op2_end(k, i)
@@ -418,7 +425,7 @@ def tile_chebyshev_l3_sparsed32_stack_pb_t_kernel(tc, z, T3, mask, x1, x2, C_w, 
                     x_q(k - 3, BOTH)
                 if k >= 2 and k + 2 < NPAIR:
                     z_q(k + 2)
-                op2(k, GP_COLS + PS_COLS, PW, nc.vector)
+                op2(k, GP_GROUPS + PS_GROUPS, 32, nc.vector)
                 if k < 2:
                     z_q(k + 2)
 

@@ -16,7 +16,7 @@ NCH = 8
 NPAIR = 16
 FLOPS = 2 * B * KIN * F + 2 * B * F * O
 
-GP_GROUPS = 17
+GP_GROUPS = 24
 PS_GROUPS = 8
 WARM = 512
 G_OF_PR = [[0], [0, 1], [0, 1], [1]]
@@ -327,7 +327,6 @@ def tile_chebyshev_l3_sparsed32_stack_pb_t_kernel(tc, z, T3, mask, x1, x2, C_w, 
             nc.sync.dma_start(out=outv[c][:, lo * O:(lo + n) * O],
                               in_=o_sb[:, lo:lo + n, :].rearrange("p j o -> p (j o)"))
 
-        mark = const.tile([P, 1], BF16, name="mark")
         mark_u = const.tile([P, 1], U32, name="mark_u")
         BOTH = [0, 1]
 
@@ -360,11 +359,8 @@ def tile_chebyshev_l3_sparsed32_stack_pb_t_kernel(tc, z, T3, mask, x1, x2, C_w, 
         for k in range(NPAIR):
             last = k == NPAIR - 1
             if k >= 1:
-                if k - 1 < 2:
-                    nc.gpsimd.tensor_copy(out=mark[:], in_=x3_sb[k - 1][:, PW - 1:PW])
-                else:
-                    codes = zc[k + 1] if k + 1 < NPAIR else xc[k - 4]
-                    nc.gpsimd.tensor_copy(out=mark_u[:], in_=codes[:, 511:512])
+                codes = zc[k + 1] if k + 1 < NPAIR else xc[k - 4]
+                nc.gpsimd.tensor_copy(out=mark_u[:], in_=codes[:, 511:512])
                 op2(k - 1, 0, GP_GROUPS, nc.gpsimd)
             if k in later_loads:
                 cx, cz = later_loads[k]
@@ -425,7 +421,6 @@ def tile_chebyshev_l3_sparsed32_stack_pb_t_kernel(tc, z, T3, mask, x1, x2, C_w, 
                     x_q(k - 3, BOTH)
                 if k >= 2 and k + 2 < NPAIR:
                     z_q(k + 2)
-                op2(k, GP_GROUPS + PS_GROUPS, 32, nc.vector)
                 if k < 2:
                     z_q(k + 2)
 

@@ -16,8 +16,9 @@ NCH = 8
 NPAIR = 16
 FLOPS = 2 * B * KIN * F + 2 * B * F * O
 
-GP_GROUPS = 24
-PS_GROUPS = 8
+GP_GROUPS = 20
+PS_RANGES = [(20, 28), (28, 32)]
+GATE_GROUPS = 8
 WARM = 512
 G_OF_PR = [[0], [0, 1], [0, 1], [1]]
 CI = {(0, 0): 0, (1, 0): 1, (2, 0): 2, (1, 1): 5, (2, 1): 6, (3, 1): 7}
@@ -161,7 +162,7 @@ def tile_chebyshev_l3_sparsed32_stack_pb_t_kernel(tc, z, T3, mask, x1, x2, C_w, 
             hh, lo = fp // 2, (fp % 2) * 2 * KIN
             ww = wm[hh][:]
             for g in range(2):
-                wt = psum.tile([P, 2, 256], F32, name="wt", tag="p3", bufs=4)
+                wt = psum.tile([P, 2, 256], F32, name="wt", tag="p3", bufs=3)
                 for u in range(2):
                     for fl in range(2):
                         col = lo // 2 + u * 512 + fl * 256 + g * P
@@ -214,7 +215,7 @@ def tile_chebyshev_l3_sparsed32_stack_pb_t_kernel(tc, z, T3, mask, x1, x2, C_w, 
         po = {}
 
         def mm1(k, pr):
-            bank = psum.tile([P, 512], F32, name="p3_%d_%d" % (k, pr), tag="p3", bufs=4)
+            bank = psum.tile([P, 512], F32, name="p3_%d_%d" % (k, pr), tag="p3", bufs=3)
             p3[(k, pr)] = bank
             gs = G_OF_PR[pr]
             for jl in range(2):
@@ -227,19 +228,17 @@ def tile_chebyshev_l3_sparsed32_stack_pb_t_kernel(tc, z, T3, mask, x1, x2, C_w, 
                         rhs=wc[:, ci * 256:(ci + 1) * 256].bitcast(FP8X4), rhs_scale=ws[:, ci * 256:(ci + 1) * 256],
                         start=(g == gs[0]), stop=(g == gs[-1]))
 
-        def op1(k, units=(0, 1)):
+        def op1(k, pr, lo=0, hi=32):
             if k not in y_sb:
                 y_sb[k] = work.tile([P, PW], F32, name="y_%d" % k, tag="y", bufs=2)
-            ss = slice(16 * units[0], 16 * units[-1] + 16)
             yv = y_sb[k][:].rearrange("p (pr s r) -> p pr s r", pr=4, r=16)
             x2u = x2_sb[k].rearrange("p (s q) -> p s q", q=64)
-            for pr in range(4):
-                nc.vector.scalar_tensor_tensor(
-                    out=yv[:, pr, ss, :],
-                    in0=p3[(k, pr)][:].rearrange("p (s r) -> p s r", r=16)[:, ss, :],
-                    scalar=2.0,
-                    in1=x2u[:, ss, pr * 16:(pr + 1) * 16],
-                    op0=ALU.mult, op1=ALU.mult)
+            nc.vector.scalar_tensor_tensor(
+                out=yv[:, pr, lo:hi, :],
+                in0=p3[(k, pr)][:].rearrange("p (s r) -> p s r", r=16)[:, lo:hi, :],
+                scalar=2.0,
+                in1=x2u[:, lo:hi, pr * 16:(pr + 1) * 16],
+                op0=ALU.mult, op1=ALU.mult)
 
         def by_pr(view):
             return view.rearrange("p (s pr r) -> p pr s r", pr=4, r=16)
@@ -257,16 +256,18 @@ def tile_chebyshev_l3_sparsed32_stack_pb_t_kernel(tc, z, T3, mask, x1, x2, C_w, 
         xb = {}
 
         def x1_bank(k):
-            xb[k] = psum.tile([P, 64 * PS_GROUPS], F32, name="xb", tag="xb", bufs=1)
-            nc.tensor.matmul(out=xb[k][:], lhsT=ident_b[:], rhs=x1_sb[k][:, 64 * GP_GROUPS:64 * (GP_GROUPS + PS_GROUPS)],
-                             start=True, stop=True)
+            for i, (lo, hi) in enumerate(PS_RANGES):
+                bank = psum.tile([P, 64 * (hi - lo)], F32, name="xb_%d" % i, tag="xb_%d" % i, bufs=1)
+                nc.tensor.matmul(out=bank[:], lhsT=ident_b[:], rhs=x1_sb[k][:, 64 * lo:64 * hi], start=True, stop=True)
+                xb[(k, i)] = bank
 
         def op2_bank(k):
-            subtract(k, GP_GROUPS, GP_GROUPS + PS_GROUPS, xb[k][:], nc.vector)
+            for i, (lo, hi) in enumerate(PS_RANGES):
+                subtract(k, lo, hi, xb[(k, i)][:], nc.vector)
 
         def op2_end(k, i):
             cols = slice(512 * i, 512 * i + 512)
-            xe = psum.tile([P, 512], F32, name="xe_%d" % i, tag="p3", bufs=4)
+            xe = psum.tile([P, 512], F32, name="xe_%d" % i, tag="p3", bufs=3)
             nc.tensor.matmul(out=xe[:], lhsT=ident_b[:], rhs=x1_sb[k][:, cols], start=True, stop=True)
             subtract(k, 8 * i, 8 * i + 8, xe[:], nc.vector)
 
@@ -280,7 +281,7 @@ def tile_chebyshev_l3_sparsed32_stack_pb_t_kernel(tc, z, T3, mask, x1, x2, C_w, 
             dst = xg[k][:].bitcast(F32).rearrange("p (v g b u) -> p v g b u", v=2, g=2, u=2)
             if split:
                 for g in range(2):
-                    xh = psum.tile([P, 2, P], F32, name="xh", tag="p3", bufs=4)
+                    xh = psum.tile([P, 2, P], F32, name="xh", tag="p3", bufs=3)
                     for u in range(2):
                         nc.tensor.transpose(xh[:, u, :], x_words(k, unit, g, u), ident_f[:])
                     if g == 0:
@@ -302,35 +303,36 @@ def tile_chebyshev_l3_sparsed32_stack_pb_t_kernel(tc, z, T3, mask, x1, x2, C_w, 
             nc.vector.quantize_mx(
                 out=xc[k][:, lo:lo + n].bitcast(FP8X4), scales=xs[k][:, lo:lo + n], in_=xg[k][:, 4 * lo:4 * (lo + n)])
 
-        def mm2(k, units):
-            c = k // 2
-            key = c if c < NCH - 1 else (k, units[0])
-            if key not in po:
-                po[key] = psum.tile([P, 4, O], F32, name="po_%d" % c,
-                                    tag=("po" if c < NCH - 1 else "p3"), bufs=(1 if c < NCH - 1 else 4))
-            for unit in units:
+        def mm2(k, units, bank=("po", 1)):
+            key = (k, units[0])
+            po[key] = psum.tile([P, len(units), O], F32, name="po_%d_%d" % key, tag=bank[0], bufs=bank[1])
+            for i, unit in enumerate(units):
                 for g in range(2):
                     lo = (unit * 2 + g) * P
                     nc.tensor.matmul_mx(
-                        out=po[key][:, (k % 2) * 2 + unit, :],
+                        out=po[key][:, i, :],
                         lhsT=xc[k][:, lo:lo + P].bitcast(FP8X4), lhsT_scale=xs[k][:, lo:lo + P],
                         rhs=cc[:, g * O:(g + 1) * O].bitcast(FP8X4), rhs_scale=cs[:, g * O:(g + 1) * O],
                         start=(g == 0), stop=(g == 1))
 
-        o_last = const.tile([P, 4, O], F32, name="o_last")
+        o_sb = {}
 
-        def fin(c, key=None, lo=0, n=4):
-            o_sb = o_last if key else work.tile([P, 4, O], F32, name="o_sb", tag="o_sb", bufs=7)
+        def fin(k, units, store):
+            c = k // 2
+            if c not in o_sb:
+                o_sb[c] = work.tile([P, 4, O], F32, name="o_sb_%d" % c, tag="o_sb", bufs=7)
+            lo, n = (k % 2) * 2 + units[0], len(units)
             nc.vector.tensor_tensor(
-                out=o_sb[:, lo:lo + n, :], in0=po[c if key is None else key][:, lo:lo + n, :],
+                out=o_sb[c][:, lo:lo + n, :], in0=po[(k, units[0])][:],
                 in1=bias_sb[:].unsqueeze(1).to_broadcast([P, n, O]), op=ALU.add)
-            nc.sync.dma_start(out=outv[c][:, lo * O:(lo + n) * O],
-                              in_=o_sb[:, lo:lo + n, :].rearrange("p j o -> p (j o)"))
+            if store:
+                first = lo + n - store
+                nc.sync.dma_start(out=outv[c][:, first * O:(lo + n) * O],
+                                  in_=o_sb[c][:, first:lo + n, :].rearrange("p j o -> p (j o)"))
 
-        mark_u = const.tile([P, 1], U32, name="mark_u")
         BOTH = [0, 1]
 
-        P3_BANK = ("p3", 4)
+        P3_BANK = ("p3", 3)
         warm_bank = psum.tile([P, WARM], F32, name="warm_bank", tag="po", bufs=1)
         busy(warm_bank[:], 6)
         w_mul(0)
@@ -350,18 +352,14 @@ def tile_chebyshev_l3_sparsed32_stack_pb_t_kernel(tc, z, T3, mask, x1, x2, C_w, 
         z_q(0)
         z_t(1, 0, P3_BANK)
         z_t(1, 1, P3_BANK)
-        for pr in range(4):
-            mm1(0, pr)
+        mm1(0, 0)
+        mm1(0, 1)
         z_t(2, 0)
         z_t(2, 1, ("xt", 1))
         z_q(1)
 
         for k in range(NPAIR):
             last = k == NPAIR - 1
-            if k >= 1:
-                codes = zc[k + 1] if k + 1 < NPAIR else xc[k - 4]
-                nc.gpsimd.tensor_copy(out=mark_u[:], in_=codes[:, 511:512])
-                op2(k - 1, 0, GP_GROUPS, nc.gpsimd)
             if k in later_loads:
                 cx, cz = later_loads[k]
                 for hf in range(2):
@@ -370,27 +368,30 @@ def tile_chebyshev_l3_sparsed32_stack_pb_t_kernel(tc, z, T3, mask, x1, x2, C_w, 
                         load_part(x1_sb, x1v, cx, hf, "x1")
                     if cz is not None:
                         load_part(z_sb, zv, cz, hf, "z")
-            if k == 0:
-                op1(0)
             if k >= 1:
                 x1_bank(k - 1)
-            if not last:
-                mm1(k + 1, 0)
-                mm1(k + 1, 1)
-            if last:
-                mm2(k - 4, BOTH)
+            mm1(k, 2)
+            op1(k, 0)
+            mm1(k, 3)
+            op1(k, 1)
+            op1(k, 2)
+            op1(k, 3, GATE_GROUPS, 32)
             if k == 1:
                 c_t()
             if k >= 2:
-                x_t(k - 2, 0, ("tp", 1) if last else ("xt", 1))
+                x_t(k - 2, 0)
             if k + 3 < NPAIR:
                 z_t(k + 3, 0)
             if k + 4 < NPAIR:
                 z_perm(k + 4)
+            if k >= 1:
+                op2_bank(k - 1)
+            if k >= 5:
+                fin(k - 5, BOTH, 4 if k % 2 == 0 else 0)
             if not last:
-                mm1(k + 1, 2)
-                mm1(k + 1, 3)
-            if 4 <= k and not last:
+                mm1(k + 1, 0)
+                mm1(k + 1, 1)
+            if k >= 4:
                 mm2(k - 4, BOTH)
             if k == 3:
                 bias_spread()
@@ -398,45 +399,39 @@ def tile_chebyshev_l3_sparsed32_stack_pb_t_kernel(tc, z, T3, mask, x1, x2, C_w, 
                 x_t(k - 2, 1)
             if k + 3 < NPAIR:
                 z_t(k + 3, 1)
-            if last:
-                op1(k, [0])
-                op1(k, [1])
-                op2(k, 0, 8, nc.gpsimd)
-                op2_bank(k - 1)
-                for i in range(1, 4):
-                    op2_end(k, i)
-                x_q(NPAIR - 4, BOTH)
-                fin(NCH - 3)
-                x_q(NPAIR - 3, BOTH)
-            else:
-                if k >= 1:
-                    op1(k)
-                if k >= 1:
-                    op2_bank(k - 1)
-                if k >= 6 and k % 2 == 0:
-                    fin((k - 6) // 2)
+            if not last:
                 if k == 2:
                     c_q()
                 if k >= 3:
                     x_q(k - 3, BOTH)
-                if k >= 2 and k + 2 < NPAIR:
+                op1(k, 3, 0, GATE_GROUPS)
+                if k + 2 < NPAIR:
                     z_q(k + 2)
-                if k < 2:
-                    z_q(k + 2)
+                op2(k, 0, GP_GROUPS, nc.gpsimd)
+            else:
+                op1(k, 3, 0, GATE_GROUPS)
 
-        x_t(NPAIR - 2, 0, ("tp", 1))
-        x_t(NPAIR - 2, 1)
-        x_t(NPAIR - 1, 0, P3_BANK)
-        x_t(NPAIR - 1, 1, P3_BANK, True)
-        mm2(NPAIR - 4, BOTH)
-        x_q(NPAIR - 2, BOTH)
-        mm2(NPAIR - 3, BOTH)
-        x_q(NPAIR - 1, [0])
-        fin(NCH - 2)
-        mm2(NPAIR - 2, BOTH)
-        mm2(NPAIR - 1, [0])
-        x_q(NPAIR - 1, [1])
-        mm2(NPAIR - 1, [1])
-        fin(NCH - 1, (NPAIR - 2, 0), 0, 2)
-        fin(NCH - 1, (NPAIR - 1, 0), 2, 1)
-        fin(NCH - 1, (NPAIR - 1, 1), 3, 1)
+        z = NPAIR - 1
+        op2(z, 0, 8, nc.gpsimd)
+        for i in range(1, 4):
+            op2_end(z, i)
+        x_q(z - 3, BOTH)
+        fin(z - 4, BOTH, 4)
+        x_q(z - 2, BOTH)
+        x_t(z - 1, 0, ("tp", 1))
+        x_t(z - 1, 1)
+        x_t(z, 0, P3_BANK)
+        x_t(z, 1, P3_BANK, True)
+        mm2(z - 3, BOTH)
+        mm2(z - 2, BOTH, P3_BANK)
+        x_q(z - 1, BOTH)
+        fin(z - 3, BOTH, 0)
+        x_q(z, [0])
+        mm2(z - 1, BOTH)
+        mm2(z, [0], P3_BANK)
+        fin(z - 2, BOTH, 4)
+        x_q(z, [1])
+        mm2(z, [1], P3_BANK)
+        fin(z - 1, BOTH, 2)
+        fin(z, [0], 1)
+        fin(z, [1], 1)

@@ -28,7 +28,7 @@ def tile_chebyshev_l3_sparsed32_stack_pb_t_kernel(tc, z, T3, mask, x1, x2, C_w, 
     nc = tc.nc
     with ExitStack() as ctx:
         const = ctx.enter_context(tc.tile_pool(name="const", bufs=1))
-        stream = ctx.enter_context(tc.tile_pool(name="stream", bufs=4))
+        stream = ctx.enter_context(tc.tile_pool(name="stream", bufs=8))
         work = ctx.enter_context(tc.tile_pool(name="work", bufs=3))
         psum = ctx.enter_context(tc.psum_pool(name="psum", bufs=1))
         ctx.enter_context(tc.manual_schedule())
@@ -44,71 +44,73 @@ def tile_chebyshev_l3_sparsed32_stack_pb_t_kernel(tc, z, T3, mask, x1, x2, C_w, 
 
         ident_b = const.tile([P, P], BF16, name="ident_b")
         make_identity(nc, ident_b[:])
+        PW = 2 * KIN
         z_sb = {}
         x1_sb = {}
         x2_sb = {}
-        PW = 2 * KIN
 
-        def load_half(dst, src, c, hf, tag):
-            t = stream.tile([P, PW], BF16, name="%s_%d_%d" % (tag, c, hf), tag=tag)
-            nc.sync.dma_start(out=t[:], in_=src[c][:, hf * PW:(hf + 1) * PW])
-            dst[2 * c + hf] = t[:]
+        def load(dst, src, k, tag):
+            t = stream.tile([P, PW], BF16, name="%s_%d" % (tag, k), tag=tag)
+            nc.sync.dma_start(out=t[:], in_=src[k // 2][:, (k % 2) * PW:(k % 2 + 1) * PW])
+            dst[k] = t[:]
 
-        parts = {}
+        def load_z(k):
+            load(z_sb, zv, k, "z")
 
-        def load_part(dst, src, c, hf, tag):
-            if (tag, c) not in parts:
-                parts[(tag, c)] = stream.tile([P, 2 * PW], BF16, name="%s_%d" % (tag, c), tag=tag)
-            t = parts[(tag, c)]
-            nc.sync.dma_start(out=t[:, hf * PW:(hf + 1) * PW], in_=src[c][:, hf * PW:(hf + 1) * PW])
-            dst[2 * c + hf] = t[:, hf * PW:(hf + 1) * PW]
+        def load_x1(k):
+            load(x1_sb, x1v, k, "x1")
 
-        def load_whole(dst, src, c, tag):
-            t = stream.tile([P, 2 * PW], BF16, name="%s_%d" % (tag, c), tag=tag)
-            nc.sync.dma_start(out=t[:], in_=src[c])
-            for hf in range(2):
-                dst[2 * c + hf] = t[:, hf * PW:(hf + 1) * PW]
+        def load_x2(k):
+            load(x2_sb, x2v, k, "x2")
 
+        still = const.tile([P, WARM], BF16, name="still")
+        nc.vector.memset(still[:], 0.0)
         mk_sb = const.tile([P, KIN], BF16, name="mk_sb")
         nc.sync.dma_start(out=mk_sb[:], in_=mask[0:P, :])
         t3h = []
         for hh in range(2):
-            t3_t = stream.tile([P, 4 * KIN], BF16, name="t3_%d" % hh, tag="x1")
+            t3_t = work.tile([P, 4 * KIN], BF16, name="t3_%d" % hh, tag="y", bufs=2)
             t3h.append(t3_t)
-        for fp in range(4):
+
+        def load_t3(fp):
             hh, lo = fp // 2, (fp % 2) * 2 * KIN
             nc.sync.dma_start(
                 out=t3h[hh][:, lo:lo + 2 * KIN].rearrange("p (f k) -> p f k", f=2),
                 in_=t3v[:, 2 * fp:2 * fp + 2, :])
-        load_half(z_sb, zv, 0, 0, "z")
+
+        for fp in range(3):
+            load_t3(fp)
         c_sb = const.tile([P, F], BF16, name="c_sb")
         ones = const.tile([P, P], BF16, name="ones")
         nc.gpsimd.memset(ones[:], 1.0)
         bias_row = const.tile([P, O], BF16, name="bias_row")
         nc.gpsimd.memset(bias_row[:], 0.0)
         bias_sb = const.tile([P, O], F32, name="bias_sb")
-        load_half(x2_sb, x2v, 0, 0, "x2")
-        load_half(z_sb, zv, 0, 1, "z")
-        load_half(z_sb, zv, 1, 0, "z")
-        load_half(x1_sb, x1v, 0, 0, "x1")
-        load_half(z_sb, zv, 1, 1, "z")
-        load_half(x2_sb, x2v, 0, 1, "x2")
-        load_part(z_sb, zv, 2, 0, "z")
-        load_half(x1_sb, x1v, 0, 1, "x1")
+        load_z(0)
+        load_t3(3)
+        load_x2(0)
+        load_z(1)
+        load_z(2)
+        load_x1(0)
+        load_x2(1)
+        load_z(3)
         nc.sync.dma_start(out=c_sb[:], in_=C_w)
         nc.sync.dma_start(out=bias_row[0:1, :], in_=C_b.unsqueeze(0))
-        load_half(x2_sb, x2v, 1, 0, "x2")
-        load_part(z_sb, zv, 2, 1, "z")
-        load_half(x1_sb, x1v, 1, 0, "x1")
-        load_half(x2_sb, x2v, 1, 1, "x2")
-        load_part(z_sb, zv, 3, 0, "z")
-        load_half(x1_sb, x1v, 1, 1, "x1")
-        load_part(z_sb, zv, 3, 1, "z")
-        later_loads = {1: (2, 4), 2: (3, 5), 3: (4, 6), 4: (5, None), 5: (None, 7), 6: (6, None), 8: (7, None)}
+        load_z(4)
+        load_x2(2)
+        load_x1(1)
+        load_z(5)
+        load_z(6)
+        load_x2(3)
+        load_x1(2)
+        load_z(7)
+        load_x2(4)
+        load_x1(3)
+        load_x1(4)
 
         def busy(bank, times=1):
             for i in range(times):
-                nc.tensor.matmul(out=bank, lhsT=mk_sb[:, 0:P], rhs=mk_sb[:, 0:WARM], start=True, stop=True)
+                nc.tensor.matmul(out=bank, lhsT=still[:, 0:P], rhs=still[:], start=True, stop=True)
 
         zg = {}
         zp = {}
@@ -143,44 +145,44 @@ def tile_chebyshev_l3_sparsed32_stack_pb_t_kernel(tc, z, T3, mask, x1, x2, C_w, 
         wc = const.tile([P, 8 * 256], U32, name="wc", align_bytes=64)
         ws = const.tile([P, 8 * 256], U8, name="ws", align_bytes=64)
         wgw = wg[:].bitcast(F32).rearrange("p (g pr s r u) -> p g s pr r u", g=2, pr=4, s=16, r=16, u=2)
+        wgv = wg[:].rearrange("p (g pr s q) -> p g pr s q", g=2, pr=4, s=16, q=64)
+        PR_OF_G = [slice(0, 3), slice(1, 4)]
 
-        wm = []
+        mt = const.tile([P, 2 * 64 * 4], BF16, name="mt", align_bytes=64)
+        mtv = mt[:].rearrange("p (g pr q) -> p g pr q", g=2, pr=4)
 
-        def w_mul(fp):
-            hh, lo = fp // 2, (fp % 2) * 2 * KIN
-            if fp % 2 == 0:
-                wm_t = work.tile([P, PW], F32, name="wm_%d" % hh, tag="y", bufs=2)
-                wm.append(wm_t)
-            dst = wm[hh][:].bitcast(BF16)[:, lo:lo + 2 * KIN]
-            nc.vector.tensor_tensor(
-                out=dst.rearrange("p (u f m e) -> p f m u e", u=2, f=2, e=2),
-                in0=t3h[hh][:, lo:lo + 2 * KIN].rearrange("p (f m u e) -> p f m u e", f=2, u=2, e=2),
-                in1=mk_sb[:].rearrange("p (m u e) -> p m u e", u=2, e=2).unsqueeze(1).to_broadcast([P, 2, 256, 2, 2]),
-                op=ALU.mult)
-
-        def w_t(fp, second_on_vector):
-            hh, lo = fp // 2, (fp % 2) * 2 * KIN
-            ww = wm[hh][:]
+        def mask_t():
+            mw = mk_sb[:].bitcast(F32)
+            mb = psum.tile([P, 4, P], F32, name="mb", tag="xt", bufs=1)
             for g in range(2):
-                wt = psum.tile([P, 2, 256], F32, name="wt", tag="p3", bufs=3)
+                for u in range(2):
+                    nc.tensor.transpose(mb[:, 2 * g + u, :], mw[:, 256 * g + u:256 * (g + 1):2], ident_f[:])
+            nc.scalar.copy(out=mt[:].bitcast(F32).rearrange("p (g c u) -> p g c u", g=2, u=2),
+                           in_=mb[:, :, 0:64].rearrange("p (g u) c -> p g c u", u=2))
+
+        def w_t(fp):
+            tw = t3h[fp // 2][:].bitcast(F32)
+            for g in range(2):
+                wt = psum.tile([P, 2, 256], F32, name="wt", tag="p3", bufs=4)
                 for u in range(2):
                     for fl in range(2):
-                        col = lo // 2 + u * 512 + fl * 256 + g * P
-                        nc.tensor.transpose(wt[:, u, fl * P:(fl + 1) * P], ww[:, col:col + P], ident_f[:])
+                        first = ((fp % 2) * 2 + fl) * 512 + 256 * g
+                        nc.tensor.transpose(wt[:, u, fl * P:(fl + 1) * P], tw[:, first + u:first + 256:2], ident_f[:])
                 src = wt[:].rearrange("p u (s pr r) -> p s pr r u", s=4, pr=4, r=16)
-                dst = wgw[:, g, 4 * fp:4 * fp + 4, :, :, :]
-                if g == 1 and second_on_vector:
-                    nc.vector.tensor_copy(out=dst, in_=src)
-                else:
-                    nc.scalar.copy(out=dst, in_=src)
+                nc.scalar.copy(out=wgw[:, g, 4 * fp:4 * fp + 4, PR_OF_G[g], :, :], in_=src[:, :, PR_OF_G[g], :, :])
 
-        def w_q(fp):
-            for pr in range(4):
+        def w_mul(fp, g):
+            part = wgv[:, g, PR_OF_G[g], 4 * fp:4 * fp + 4, :]
+            nc.vector.tensor_tensor(
+                out=part, in0=part, in1=mtv[:, g, PR_OF_G[g], :].unsqueeze(2).to_broadcast([P, 3, 4, 64]), op=ALU.mult)
+
+        def w_q(fp, prs):
+            for pr in prs:
                 for g in G_OF_PR[pr]:
                     lo_w = CI[(pr, g)] * 256 + 64 * fp
                     nc.vector.quantize_mx(
-                        out=wc[:, lo_w:lo_w + 64].bitcast(FP8X4), scales=ws[:, lo_w:lo_w + 64],
-                        in_=wg[:, 4 * lo_w:4 * lo_w + 256])
+                        out=wc[:, lo_w:lo_w + 128].bitcast(FP8X4), scales=ws[:, lo_w:lo_w + 128],
+                        in_=wg[:, 4 * lo_w:4 * (lo_w + 128)])
 
         cg = const.tile([P, 2 * O * 4], BF16, name="cg", align_bytes=64)
         cc = const.tile([P, 2 * O], U32, name="cc", align_bytes=64)
@@ -191,11 +193,14 @@ def tile_chebyshev_l3_sparsed32_stack_pb_t_kernel(tc, z, T3, mask, x1, x2, C_w, 
             nc.tensor.matmul(out=bt[:], lhsT=ones[:], rhs=bias_row[:], start=True, stop=True)
             nc.scalar.copy(out=bias_sb[:], in_=bt[:])
 
-        def c_t():
-            cw = const.tile([P, F // 2], F32, name="cw")
+        cw = const.tile([P, F // 2], F32, name="cw")
+
+        def c_perm():
             nc.scalar.copy(out=cw[:].rearrange("p (pr s w) -> p pr s w", pr=4, w=8),
                            in_=c_sb[:].bitcast(F32).rearrange("p (s pr w) -> p pr s w", pr=4, w=8))
-            ct = psum.tile([P, 4, P], F32, name="ct", tag="xt", bufs=1)
+
+        def c_t():
+            ct = psum.tile([P, 4, P], F32, name="ct", tag="po", bufs=1)
             for g in range(2):
                 for u in range(2):
                     nc.tensor.transpose(ct[:, 2 * g + u, :], cw[:, (2 * g + u) * P:(2 * g + u + 1) * P], ident_f[:])
@@ -215,7 +220,7 @@ def tile_chebyshev_l3_sparsed32_stack_pb_t_kernel(tc, z, T3, mask, x1, x2, C_w, 
         po = {}
 
         def mm1(k, pr):
-            bank = psum.tile([P, 512], F32, name="p3_%d_%d" % (k, pr), tag="p3", bufs=3)
+            bank = psum.tile([P, 512], F32, name="p3_%d_%d" % (k, pr), tag="p3", bufs=4)
             p3[(k, pr)] = bank
             gs = G_OF_PR[pr]
             for jl in range(2):
@@ -255,21 +260,23 @@ def tile_chebyshev_l3_sparsed32_stack_pb_t_kernel(tc, z, T3, mask, x1, x2, C_w, 
 
         xb = {}
 
-        def x1_bank(k):
-            for i, (lo, hi) in enumerate(PS_RANGES):
-                bank = psum.tile([P, 64 * (hi - lo)], F32, name="xb_%d" % i, tag="xb_%d" % i, bufs=1)
-                nc.tensor.matmul(out=bank[:], lhsT=ident_b[:], rhs=x1_sb[k][:, 64 * lo:64 * hi], start=True, stop=True)
-                xb[(k, i)] = bank
+        def x1_bank(k, i):
+            lo, hi = PS_RANGES[i]
+            xb[k] = psum.tile([P, 64 * (hi - lo)], F32, name="xb_%d" % i, tag="xb", bufs=1)
+            nc.tensor.matmul(out=xb[k][:], lhsT=ident_b[:], rhs=x1_sb[k][:, 64 * lo:64 * hi], start=True, stop=True)
 
-        def op2_bank(k):
-            for i, (lo, hi) in enumerate(PS_RANGES):
-                subtract(k, lo, hi, xb[(k, i)][:], nc.vector)
+        def op2_bank(k, i):
+            lo, hi = PS_RANGES[i]
+            subtract(k, lo, hi, xb[k][:], nc.vector)
+
+        xe = {}
+
+        def x1_end(k, i):
+            xe[i] = psum.tile([P, 512], F32, name="xe_%d" % i, tag="p3", bufs=4)
+            nc.tensor.matmul(out=xe[i][:], lhsT=ident_b[:], rhs=x1_sb[k][:, 512 * i:512 * i + 512], start=True, stop=True)
 
         def op2_end(k, i):
-            cols = slice(512 * i, 512 * i + 512)
-            xe = psum.tile([P, 512], F32, name="xe_%d" % i, tag="p3", bufs=3)
-            nc.tensor.matmul(out=xe[:], lhsT=ident_b[:], rhs=x1_sb[k][:, cols], start=True, stop=True)
-            subtract(k, 8 * i, 8 * i + 8, xe[:], nc.vector)
+            subtract(k, 8 * i, 8 * i + 8, xe[i][:], nc.vector)
 
         def x_words(k, unit, g, u):
             first = (2 * g + u) * 256 + unit * P
@@ -281,7 +288,7 @@ def tile_chebyshev_l3_sparsed32_stack_pb_t_kernel(tc, z, T3, mask, x1, x2, C_w, 
             dst = xg[k][:].bitcast(F32).rearrange("p (v g b u) -> p v g b u", v=2, g=2, u=2)
             if split:
                 for g in range(2):
-                    xh = psum.tile([P, 2, P], F32, name="xh", tag="p3", bufs=3)
+                    xh = psum.tile([P, 2, P], F32, name="xh", tag="p3", bufs=4)
                     for u in range(2):
                         nc.tensor.transpose(xh[:, u, :], x_words(k, unit, g, u), ident_f[:])
                     if g == 0:
@@ -332,106 +339,168 @@ def tile_chebyshev_l3_sparsed32_stack_pb_t_kernel(tc, z, T3, mask, x1, x2, C_w, 
 
         BOTH = [0, 1]
 
-        P3_BANK = ("p3", 3)
+        P3_BANK = ("p3", 4)
         warm_bank = psum.tile([P, WARM], F32, name="warm_bank", tag="po", bufs=1)
-        busy(warm_bank[:], 6)
-        w_mul(0)
-        w_mul(1)
-        w_t(0, False)
-        w_mul(2)
-        w_t(1, False)
-        w_mul(3)
-        w_t(2, True)
-        w_q(0)
-        w_t(3, True)
-        w_q(1)
-        z_t(0, 0, P3_BANK)
-        z_t(0, 1, P3_BANK)
-        w_q(2)
-        w_q(3)
+        busy(warm_bank[:], 5)
+        mask_t()
+        w_t(0)
+        w_mul(0, 0)
+        w_mul(0, 1)
+        w_t(1)
+        w_mul(1, 0)
+        w_mul(1, 1)
+        w_t(2)
+        w_q(0, range(4))
+        w_mul(2, 0)
+        w_mul(2, 1)
+        z_t(0, 0, ("tp", 1))
+        z_t(0, 1, ("xt", 1))
+        w_t(3)
         z_q(0)
-        z_t(1, 0, P3_BANK)
-        z_t(1, 1, P3_BANK)
+        w_mul(3, 0)
+        w_mul(3, 1)
+        w_q(2, [0])
+        z_t(1, 0, ("tp", 1))
+        z_t(1, 1, ("xt", 1))
         mm1(0, 0)
-        mm1(0, 1)
+        w_q(2, [1, 2, 3])
+        for pr in range(1, 4):
+            mm1(0, pr)
+
+        def load_ahead(k):
+            if k + 5 < NPAIR:
+                load_x2(k + 5)
+                load_x1(k + 5)
+            if k + 8 < NPAIR:
+                load_z(k + 8)
+
+        load_ahead(0)
+        op1(0, 0)
+        op1(0, 1)
         z_t(2, 0)
         z_t(2, 1, ("xt", 1))
         z_q(1)
+        mm1(1, 0)
+        mm1(1, 1)
+        x1_bank(0, 0)
+        op1(0, 2)
+        op1(0, 3)
+        mm1(1, 2)
+        mm1(1, 3)
+        op2(0, 0, GP_GROUPS, nc.gpsimd)
+        load_ahead(1)
+        op1(1, 0)
+        c_perm()
+        z_perm(4)
+        z_t(3, 0)
+        z_t(3, 1, ("xt", 1))
+        c_t()
+        z_perm(5)
+        op2_bank(0, 0)
+        x1_bank(0, 1)
+        op1(1, 1)
+        op1(1, 2)
+        op1(1, 3, GATE_GROUPS, 32)
+        op2_bank(0, 1)
+        x1_bank(1, 0)
+        z_q(2)
+        for pr in range(3):
+            mm1(2, pr)
+        op1(1, 3, 0, GATE_GROUPS)
+        z_q(3)
+        op2(1, 0, GP_GROUPS, nc.gpsimd)
+        load_ahead(2)
+        mm1(2, 3)
+        op1(2, 0)
+        z_t(4, 0)
+        z_t(4, 1, ("xt", 1))
+        op1(2, 1)
+        op2_bank(1, 0)
+        x1_bank(1, 1)
+        mm1(3, 0)
+        mm1(3, 1)
+        op1(2, 2)
+        op1(2, 3, GATE_GROUPS, 32)
+        z_t(5, 0)
+        z_t(5, 1, ("po", 1))
+        x_t(0, 0)
+        mm1(3, 2)
+        op2_bank(1, 1)
+        x1_bank(2, 0)
+        op1(2, 3, 0, GATE_GROUPS)
+        z_q(4)
+        op2(2, 0, GP_GROUPS, nc.gpsimd)
 
-        for k in range(NPAIR):
+        for k in range(3, NPAIR):
             last = k == NPAIR - 1
-            if k in later_loads:
-                cx, cz = later_loads[k]
-                for hf in range(2):
-                    if cx is not None:
-                        load_part(x2_sb, x2v, cx, hf, "x2")
-                        load_part(x1_sb, x1v, cx, hf, "x1")
-                    if cz is not None:
-                        load_part(z_sb, zv, cz, hf, "z")
-            if k >= 1:
-                x1_bank(k - 1)
-            mm1(k, 2)
+            load_ahead(k)
             op1(k, 0)
+            if k >= 5:
+                fin(k - 5, BOTH, 4 if k % 2 == 0 else 0)
             mm1(k, 3)
-            op1(k, 1)
-            op1(k, 2)
-            op1(k, 3, GATE_GROUPS, 32)
-            if k == 1:
-                c_t()
-            if k >= 2:
-                x_t(k - 2, 0)
+            if k == 3:
+                x_t(0, 1, ("po", 1))
+            x_t(k - 2, 0)
             if k + 3 < NPAIR:
                 z_t(k + 3, 0)
             if k + 4 < NPAIR:
                 z_perm(k + 4)
-            if k >= 1:
-                op2_bank(k - 1)
-            if k >= 5:
-                fin(k - 5, BOTH, 4 if k % 2 == 0 else 0)
             if not last:
                 mm1(k + 1, 0)
+            op1(k, 1)
+            if not last:
                 mm1(k + 1, 1)
+            op2_bank(k - 1, 0)
+            x1_bank(k - 1, 1)
+            op1(k, 2)
+            op1(k, 3, GATE_GROUPS, 32)
+            if last:
+                for i in range(1, 4):
+                    x1_end(k, i)
+            x_t(k - 2, 1)
+            if k + 3 < NPAIR:
+                z_t(k + 3, 1)
+            if not last:
+                mm1(k + 1, 2)
             if k >= 4:
                 mm2(k - 4, BOTH)
             if k == 3:
                 bias_spread()
-            if k >= 2:
-                x_t(k - 2, 1)
-            if k + 3 < NPAIR:
-                z_t(k + 3, 1)
+            op2_bank(k - 1, 1)
             if not last:
-                if k == 2:
+                x1_bank(k, 0)
+                if k == 3:
                     c_q()
-                if k >= 3:
-                    x_q(k - 3, BOTH)
+                x_q(k - 3, BOTH)
                 op1(k, 3, 0, GATE_GROUPS)
-                if k + 2 < NPAIR:
+                if k == NPAIR - 2:
+                    x_q(k - 2, BOTH)
+                elif k + 2 < NPAIR:
                     z_q(k + 2)
                 op2(k, 0, GP_GROUPS, nc.gpsimd)
             else:
                 op1(k, 3, 0, GATE_GROUPS)
 
-        z = NPAIR - 1
-        op2(z, 0, 8, nc.gpsimd)
+        e = NPAIR - 1
+        op2(e, 0, 8, nc.gpsimd)
+        mm2(e - 3, BOTH, P3_BANK)
+        x_t(e - 1, 0, ("tp", 1))
+        x_t(e - 1, 1)
         for i in range(1, 4):
-            op2_end(z, i)
-        x_q(z - 3, BOTH)
-        fin(z - 4, BOTH, 4)
-        x_q(z - 2, BOTH)
-        x_t(z - 1, 0, ("tp", 1))
-        x_t(z - 1, 1)
-        x_t(z, 0, P3_BANK)
-        x_t(z, 1, P3_BANK, True)
-        mm2(z - 3, BOTH)
-        mm2(z - 2, BOTH, P3_BANK)
-        x_q(z - 1, BOTH)
-        fin(z - 3, BOTH, 0)
-        x_q(z, [0])
-        mm2(z - 1, BOTH)
-        mm2(z, [0], P3_BANK)
-        fin(z - 2, BOTH, 4)
-        x_q(z, [1])
-        mm2(z, [1], P3_BANK)
-        fin(z - 1, BOTH, 2)
-        fin(z, [0], 1)
-        fin(z, [1], 1)
+            op2_end(e, i)
+        fin(e - 4, BOTH, 4)
+        x_q(e - 2, BOTH)
+        x_t(e, 0, P3_BANK)
+        x_t(e, 1, P3_BANK, True)
+        mm2(e - 2, BOTH)
+        fin(e - 3, BOTH, 0)
+        x_q(e - 1, BOTH)
+        x_q(e, [0])
+        mm2(e - 1, BOTH, P3_BANK)
+        fin(e - 2, BOTH, 4)
+        mm2(e, [0], P3_BANK)
+        x_q(e, [1])
+        fin(e - 1, BOTH, 2)
+        mm2(e, [1], ("po", 1))
+        fin(e, [0], 1)
+        fin(e, [1], 1)

@@ -9,6 +9,7 @@ U32 = mybir.dt.uint32
 U8 = mybir.dt.uint8
 FP8X4 = mybir.dt.float8_e4m3fn_x4
 ALU = mybir.AluOpType
+ACTF = mybir.ActivationFunctionType
 
 P = 128
 B, KIN, F, O = 4096, 1024, 1024, 128
@@ -19,6 +20,7 @@ FLOPS = 2 * B * KIN * F + 2 * B * F * O
 GP_GROUPS = 20
 PS_RANGES = [(20, 28), (28, 32)]
 GATE_GROUPS = 8
+VECTOR_BIAS = 12
 WARM = 512
 G_OF_PR = [[0], [0, 1], [0, 1], [1]]
 CI = {(0, 0): 0, (1, 0): 1, (2, 0): 2, (1, 1): 5, (2, 1): 6, (3, 1): 7}
@@ -86,6 +88,7 @@ def tile_chebyshev_l3_sparsed32_stack_pb_t_kernel(tc, z, T3, mask, x1, x2, C_w, 
         bias_row = const.tile([P, O], BF16, name="bias_row")
         nc.gpsimd.memset(bias_row[:], 0.0)
         bias_sb = const.tile([P, O], F32, name="bias_sb")
+        bias_col = const.tile([P, 2], F32, name="bias_col")
         load_z(0)
         load_t3(3)
         load_x2(0)
@@ -193,6 +196,11 @@ def tile_chebyshev_l3_sparsed32_stack_pb_t_kernel(tc, z, T3, mask, x1, x2, C_w, 
             nc.tensor.matmul(out=bt[:], lhsT=ones[:], rhs=bias_row[:], start=True, stop=True)
             nc.scalar.copy(out=bias_sb[:], in_=bt[:])
 
+        def bias_turn():
+            bt = psum.tile([P, 2], F32, name="bc", tag="po", bufs=1)
+            nc.tensor.matmul(out=bt[:], lhsT=bias_row[:], rhs=ones[:, 0:2], start=True, stop=True)
+            nc.scalar.copy(out=bias_col[:], in_=bt[:])
+
         cw = const.tile([P, F // 2], F32, name="cw")
 
         def c_perm():
@@ -285,7 +293,11 @@ def tile_chebyshev_l3_sparsed32_stack_pb_t_kernel(tc, z, T3, mask, x1, x2, C_w, 
         def x_t(k, unit, bank=("xt", 1), split=False):
             if unit == 0:
                 xg[k] = work.tile([P, 2 * 1024], BF16, name="xg_%d" % k, tag="xg", bufs=3, align_bytes=64)
-            dst = xg[k][:].bitcast(F32).rearrange("p (v g b u) -> p v g b u", v=2, g=2, u=2)
+            words = xg[k][:].bitcast(F32)
+            if k < VECTOR_BIAS:
+                dst = words.rearrange("p (g v b u) -> p v g b u", v=2, g=2, u=2)
+            else:
+                dst = words.rearrange("p (v g b u) -> p v g b u", v=2, g=2, u=2)
             if split:
                 for g in range(2):
                     xh = psum.tile([P, 2, P], F32, name="xh", tag="p3", bufs=4)
@@ -322,7 +334,32 @@ def tile_chebyshev_l3_sparsed32_stack_pb_t_kernel(tc, z, T3, mask, x1, x2, C_w, 
                         rhs=cc[:, g * O:(g + 1) * O].bitcast(FP8X4), rhs_scale=cs[:, g * O:(g + 1) * O],
                         start=(g == 0), stop=(g == 1))
 
+        pt = {}
+        ot = {}
+
+        def mm2_t(k):
+            pt[k] = psum.tile([P, 2, 256], F32, name="pt_%d" % k, tag="po", bufs=1)
+            for g in range(2):
+                nc.tensor.matmul_mx(
+                    out=pt[k][:, 0, :],
+                    lhsT=cc[:, g * O:(g + 1) * O].bitcast(FP8X4), lhsT_scale=cs[:, g * O:(g + 1) * O],
+                    rhs=xc[k][:, 256 * g:256 * (g + 1)].bitcast(FP8X4), rhs_scale=xs[k][:, 256 * g:256 * (g + 1)],
+                    start=(g == 0), stop=(g == 1))
+            ot[k] = work.tile([P, 256], F32, name="ot_%d" % k, tag="ot", bufs=2)
+            nc.scalar.activation(out=ot[k][:], in_=pt[k][:, 0, :], func=ACTF.Identity, bias=bias_col[:, 0:1], scale=1.0)
+
         o_sb = {}
+
+        def out_t(k):
+            c = k // 2
+            for unit in range(2):
+                nc.tensor.transpose(pt[k][:, 1, unit * P:(unit + 1) * P], ot[k][:, unit * P:(unit + 1) * P], ident_f[:])
+            if c not in o_sb:
+                o_sb[c] = work.tile([P, 4, O], F32, name="o_sb_%d" % c, tag="o_sb", bufs=7)
+            lo = (k % 2) * 2
+            nc.scalar.copy(out=o_sb[c][:, lo:lo + 2, :].rearrange("p j o -> p (j o)"), in_=pt[k][:, 1, :])
+            if k % 2 == 1:
+                nc.sync.dma_start(out=outv[c], in_=o_sb[c][:].rearrange("p j o -> p (j o)"))
 
         def fin(k, units, store):
             c = k // 2
@@ -435,23 +472,27 @@ def tile_chebyshev_l3_sparsed32_stack_pb_t_kernel(tc, z, T3, mask, x1, x2, C_w, 
             last = k == NPAIR - 1
             load_ahead(k)
             op1(k, 0)
-            if k >= 5:
-                fin(k - 5, BOTH, 4 if k % 2 == 0 else 0)
             mm1(k, 3)
             if k == 3:
                 x_t(0, 1, ("po", 1))
             x_t(k - 2, 0)
             if k + 3 < NPAIR:
                 z_t(k + 3, 0)
+            if k >= 5:
+                out_t(k - 5)
             if k + 4 < NPAIR:
                 z_perm(k + 4)
+            if k == 3:
+                op2_bank(k - 1, 0)
+                x1_bank(k - 1, 1)
             if not last:
                 mm1(k + 1, 0)
             op1(k, 1)
             if not last:
                 mm1(k + 1, 1)
-            op2_bank(k - 1, 0)
-            x1_bank(k - 1, 1)
+            if k > 3:
+                op2_bank(k - 1, 0)
+                x1_bank(k - 1, 1)
             op1(k, 2)
             op1(k, 3, GATE_GROUPS, 32)
             if last:
@@ -463,9 +504,10 @@ def tile_chebyshev_l3_sparsed32_stack_pb_t_kernel(tc, z, T3, mask, x1, x2, C_w, 
             if not last:
                 mm1(k + 1, 2)
             if k >= 4:
-                mm2(k - 4, BOTH)
+                mm2_t(k - 4)
             if k == 3:
                 bias_spread()
+                bias_turn()
             op2_bank(k - 1, 1)
             if not last:
                 x1_bank(k, 0)
@@ -483,24 +525,24 @@ def tile_chebyshev_l3_sparsed32_stack_pb_t_kernel(tc, z, T3, mask, x1, x2, C_w, 
 
         e = NPAIR - 1
         op2(e, 0, 8, nc.gpsimd)
-        mm2(e - 3, BOTH, P3_BANK)
         x_t(e - 1, 0, ("tp", 1))
         x_t(e - 1, 1)
+        out_t(e - 4)
+        mm2(e - 3, BOTH, P3_BANK)
         for i in range(1, 4):
             op2_end(e, i)
-        fin(e - 4, BOTH, 4)
         x_q(e - 2, BOTH)
+        fin(e - 3, BOTH, 0)
         x_t(e, 0, P3_BANK)
         x_t(e, 1, P3_BANK, True)
         mm2(e - 2, BOTH)
-        fin(e - 3, BOTH, 0)
         x_q(e - 1, BOTH)
+        fin(e - 2, BOTH, 4)
         x_q(e, [0])
         mm2(e - 1, BOTH, P3_BANK)
-        fin(e - 2, BOTH, 4)
         mm2(e, [0], P3_BANK)
         x_q(e, [1])
         fin(e - 1, BOTH, 2)
-        mm2(e, [1], ("po", 1))
+        mm2(e, [1], P3_BANK)
         fin(e, [0], 1)
         fin(e, [1], 1)

@@ -67,8 +67,8 @@ def tile_chebyshev_l3_sparsed32_stack_pb_t_kernel(tc, z, T3, mask, x1, x2, C_w, 
 
         still = const.tile([P, WARM], BF16, name="still")
         nc.vector.memset(still[:], 0.0)
-        mk_sb = const.tile([P, KIN], BF16, name="mk_sb")
-        nc.sync.dma_start(out=mk_sb[:], in_=mask[0:P, :])
+        mk_sb = const.tile([P, KIN // 2], BF16, name="mk_sb")
+        nc.sync.dma_start(out=mk_sb[:], in_=mask[0:64, :].rearrange("c (g k) -> (c g) k", g=2))
         t3h = []
         for hh in range(2):
             t3_t = work.tile([P, 4 * KIN], BF16, name="t3_%d" % hh, tag="y", bufs=2)
@@ -97,18 +97,17 @@ def tile_chebyshev_l3_sparsed32_stack_pb_t_kernel(tc, z, T3, mask, x1, x2, C_w, 
         load_x1(0)
         load_x2(1)
         load_z(3)
-        nc.sync.dma_start(out=c_sb[:], in_=C_w)
-        nc.sync.dma_start(out=bias_row[0:1, :], in_=C_b.unsqueeze(0))
-        load_z(4)
         load_x2(2)
         load_x1(1)
-        load_z(5)
-        load_z(6)
+        load_z(4)
         load_x2(3)
         load_x1(2)
-        load_z(7)
+        nc.sync.dma_start(out=c_sb[:], in_=C_w)
+        nc.sync.dma_start(out=bias_row[0:1, :], in_=C_b.unsqueeze(0))
+        load_z(5)
         load_x2(4)
         load_x1(3)
+        load_z(6)
         load_x1(4)
 
         def busy(bank, times=1):
@@ -120,12 +119,11 @@ def tile_chebyshev_l3_sparsed32_stack_pb_t_kernel(tc, z, T3, mask, x1, x2, C_w, 
         zc = {}
         zs = {}
 
-        def z_t(k, g, early=None):
+        def z_t(k, g):
             if g == 0:
                 zg[k] = work.tile([P, 2 * 256 * 4], BF16, name="zg_%d" % k, tag="zg", align_bytes=64)
             zw = zp[k][:] if k in zp else z_sb[k].bitcast(F32)
-            tag, bufs = early if early else ("tp", 1)
-            zt = psum.tile([P, 2, 256], F32, name="zt", tag=tag, bufs=bufs)
+            zt = psum.tile([P, 2, 256], F32, name="zt", tag="tt", bufs=2)
             for u in range(2):
                 for jl in range(2):
                     col = jl * 512 + 256 * g
@@ -156,12 +154,11 @@ def tile_chebyshev_l3_sparsed32_stack_pb_t_kernel(tc, z, T3, mask, x1, x2, C_w, 
 
         def mask_t():
             mw = mk_sb[:].bitcast(F32)
-            mb = psum.tile([P, 4, P], F32, name="mb", tag="xt", bufs=1)
-            for g in range(2):
-                for u in range(2):
-                    nc.tensor.transpose(mb[:, 2 * g + u, :], mw[:, 256 * g + u:256 * (g + 1):2], ident_f[:])
+            mb = psum.tile([P, 2, P], F32, name="mb", tag="tt", bufs=2)
+            for u in range(2):
+                nc.tensor.transpose(mb[:, u, :], mw[:, u:256:2], ident_f[:])
             nc.scalar.copy(out=mt[:].bitcast(F32).rearrange("p (g c u) -> p g c u", g=2, u=2),
-                           in_=mb[:, :, 0:64].rearrange("p (g u) c -> p g c u", u=2))
+                           in_=mb[:].rearrange("p u (c g) -> p g c u", g=2))
 
         def w_t(fp):
             tw = t3h[fp // 2][:].bitcast(F32)
@@ -192,14 +189,11 @@ def tile_chebyshev_l3_sparsed32_stack_pb_t_kernel(tc, z, T3, mask, x1, x2, C_w, 
         cs = const.tile([P, 2 * O], U8, name="cs", align_bytes=64)
 
         def bias_spread():
-            bt = psum.tile([P, O], F32, name="bt", tag="po", bufs=1)
-            nc.tensor.matmul(out=bt[:], lhsT=ones[:], rhs=bias_row[:], start=True, stop=True)
-            nc.scalar.copy(out=bias_sb[:], in_=bt[:])
-
-        def bias_turn():
-            bt = psum.tile([P, 2], F32, name="bc", tag="po", bufs=1)
-            nc.tensor.matmul(out=bt[:], lhsT=bias_row[:], rhs=ones[:, 0:2], start=True, stop=True)
-            nc.scalar.copy(out=bias_col[:], in_=bt[:])
+            bt = psum.tile([P, O + 2], F32, name="bt", tag="po", bufs=1)
+            nc.tensor.matmul(out=bt[:, 0:O], lhsT=ones[:], rhs=bias_row[:], start=True, stop=True)
+            nc.tensor.matmul(out=bt[:, O:O + 2], lhsT=bias_row[:], rhs=ones[:, 0:2], start=True, stop=True)
+            nc.scalar.copy(out=bias_sb[:], in_=bt[:, 0:O])
+            nc.scalar.copy(out=bias_col[:], in_=bt[:, O:O + 2])
 
         cw = const.tile([P, F // 2], F32, name="cw")
 
@@ -290,7 +284,7 @@ def tile_chebyshev_l3_sparsed32_stack_pb_t_kernel(tc, z, T3, mask, x1, x2, C_w, 
             first = (2 * g + u) * 256 + unit * P
             return x3_sb[k][:].bitcast(F32)[:, first:first + P]
 
-        def x_t(k, unit, bank=("xt", 1), split=False):
+        def x_t(k, unit, bank=("tt", 2), split=False):
             if unit == 0:
                 xg[k] = work.tile([P, 2 * 1024], BF16, name="xg_%d" % k, tag="xg", bufs=3, align_bytes=64)
             words = xg[k][:].bitcast(F32)
@@ -337,8 +331,8 @@ def tile_chebyshev_l3_sparsed32_stack_pb_t_kernel(tc, z, T3, mask, x1, x2, C_w, 
         pt = {}
         ot = {}
 
-        def mm2_t(k):
-            pt[k] = psum.tile([P, 2, 256], F32, name="pt_%d" % k, tag="po", bufs=1)
+        def mm2_t(k, bank=("po", 1)):
+            pt[k] = psum.tile([P, 2, 256], F32, name="pt_%d" % k, tag=bank[0], bufs=bank[1])
             for g in range(2):
                 nc.tensor.matmul_mx(
                     out=pt[k][:, 0, :],
@@ -390,107 +384,51 @@ def tile_chebyshev_l3_sparsed32_stack_pb_t_kernel(tc, z, T3, mask, x1, x2, C_w, 
         w_q(0, range(4))
         w_mul(2, 0)
         w_mul(2, 1)
-        z_t(0, 0, ("tp", 1))
-        z_t(0, 1, ("xt", 1))
+        z_t(0, 0)
+        z_t(0, 1)
         w_t(3)
         z_q(0)
         w_mul(3, 0)
         w_mul(3, 1)
         w_q(2, [0])
-        z_t(1, 0, ("tp", 1))
-        z_t(1, 1, ("xt", 1))
+        z_t(1, 0)
+        z_t(1, 1)
         mm1(0, 0)
         w_q(2, [1, 2, 3])
-        for pr in range(1, 4):
+        for pr in range(1, 3):
             mm1(0, pr)
 
-        def load_ahead(k):
+        for k in range(NPAIR):
+            last = k == NPAIR - 1
             if k + 5 < NPAIR:
                 load_x2(k + 5)
                 load_x1(k + 5)
-            if k + 8 < NPAIR:
-                load_z(k + 8)
-
-        load_ahead(0)
-        op1(0, 0)
-        op1(0, 1)
-        z_t(2, 0)
-        z_t(2, 1, ("xt", 1))
-        z_q(1)
-        mm1(1, 0)
-        mm1(1, 1)
-        x1_bank(0, 0)
-        op1(0, 2)
-        op1(0, 3)
-        mm1(1, 2)
-        mm1(1, 3)
-        op2(0, 0, GP_GROUPS, nc.gpsimd)
-        load_ahead(1)
-        op1(1, 0)
-        c_perm()
-        z_perm(4)
-        z_t(3, 0)
-        z_t(3, 1, ("xt", 1))
-        c_t()
-        z_perm(5)
-        op2_bank(0, 0)
-        x1_bank(0, 1)
-        op1(1, 1)
-        op1(1, 2)
-        op1(1, 3, GATE_GROUPS, 32)
-        op2_bank(0, 1)
-        x1_bank(1, 0)
-        z_q(2)
-        for pr in range(3):
-            mm1(2, pr)
-        op1(1, 3, 0, GATE_GROUPS)
-        z_q(3)
-        op2(1, 0, GP_GROUPS, nc.gpsimd)
-        load_ahead(2)
-        mm1(2, 3)
-        op1(2, 0)
-        z_t(4, 0)
-        z_t(4, 1, ("xt", 1))
-        op1(2, 1)
-        op2_bank(1, 0)
-        x1_bank(1, 1)
-        mm1(3, 0)
-        mm1(3, 1)
-        op1(2, 2)
-        op1(2, 3, GATE_GROUPS, 32)
-        z_t(5, 0)
-        z_t(5, 1, ("po", 1))
-        x_t(0, 0)
-        mm1(3, 2)
-        op2_bank(1, 1)
-        x1_bank(2, 0)
-        op1(2, 3, 0, GATE_GROUPS)
-        z_q(4)
-        op2(2, 0, GP_GROUPS, nc.gpsimd)
-
-        for k in range(3, NPAIR):
-            last = k == NPAIR - 1
-            load_ahead(k)
+            if k + 7 < NPAIR:
+                load_z(k + 7)
             op1(k, 0)
             mm1(k, 3)
-            if k == 3:
-                x_t(0, 1, ("po", 1))
-            x_t(k - 2, 0)
-            if k + 3 < NPAIR:
-                z_t(k + 3, 0)
             if k >= 5:
-                out_t(k - 5)
-            if k + 4 < NPAIR:
-                z_perm(k + 4)
-            if k == 3:
-                op2_bank(k - 1, 0)
-                x1_bank(k - 1, 1)
+                mm2_t(k - 5)
+            if k + 2 < NPAIR:
+                z_t(k + 2, 0)
+                z_t(k + 2, 1)
+            else:
+                x_t(k - 2, 0)
+                x_t(k - 2, 1)
+            if k == 2:
+                c_perm()
+            if 4 <= k and k + 3 < NPAIR:
+                z_perm(k + 3)
+            if k == 0:
+                op1(k, 1)
+                z_q(1)
             if not last:
                 mm1(k + 1, 0)
-            op1(k, 1)
+            if k > 0:
+                op1(k, 1)
             if not last:
                 mm1(k + 1, 1)
-            if k > 3:
+            if k >= 1:
                 op2_bank(k - 1, 0)
                 x1_bank(k - 1, 1)
             op1(k, 2)
@@ -498,26 +436,33 @@ def tile_chebyshev_l3_sparsed32_stack_pb_t_kernel(tc, z, T3, mask, x1, x2, C_w, 
             if last:
                 for i in range(1, 4):
                     x1_end(k, i)
-            x_t(k - 2, 1)
-            if k + 3 < NPAIR:
-                z_t(k + 3, 1)
+            if last:
+                mm2_t(k - 4, P3_BANK)
+            if k >= 5:
+                out_t(k - 5)
+            if 2 <= k < NPAIR - 2:
+                x_t(k - 2, 0)
+                x_t(k - 2, 1)
+            if k == 3:
+                c_t()
+            if k == 4:
+                bias_spread()
             if not last:
                 mm1(k + 1, 2)
-            if k >= 4:
-                mm2_t(k - 4)
-            if k == 3:
-                bias_spread()
-                bias_turn()
-            op2_bank(k - 1, 1)
+            if k >= 1:
+                op2_bank(k - 1, 1)
             if not last:
                 x1_bank(k, 0)
-                if k == 3:
+                if k == 4:
                     c_q()
-                x_q(k - 3, BOTH)
+                if k >= 3:
+                    x_q(k - 3, BOTH)
+                if k == 0:
+                    z_q(2)
                 op1(k, 3, 0, GATE_GROUPS)
                 if k == NPAIR - 2:
                     x_q(k - 2, BOTH)
-                elif k + 2 < NPAIR:
+                elif 0 < k and k + 2 < NPAIR:
                     z_q(k + 2)
                 op2(k, 0, GP_GROUPS, nc.gpsimd)
             else:
@@ -525,10 +470,10 @@ def tile_chebyshev_l3_sparsed32_stack_pb_t_kernel(tc, z, T3, mask, x1, x2, C_w, 
 
         e = NPAIR - 1
         op2(e, 0, 8, nc.gpsimd)
-        x_t(e - 1, 0, ("tp", 1))
-        x_t(e - 1, 1)
         out_t(e - 4)
-        mm2(e - 3, BOTH, P3_BANK)
+        x_t(e - 1, 0)
+        x_t(e - 1, 1)
+        mm2(e - 3, BOTH)
         for i in range(1, 4):
             op2_end(e, i)
         x_q(e - 2, BOTH)

@@ -91,8 +91,8 @@ def tile_chebyshev_l3_sparsed32_stack_pb_t_kernel(tc, z, T3, mask, x1, x2, C_w, 
         bias_col = const.tile([P, 2], F32, name="bias_col")
         load_z(0)
         load_t3(3)
-        load_x2(0)
         load_z(1)
+        load_x2(0)
         load_z(2)
         load_x1(0)
         load_x2(1)
@@ -297,10 +297,7 @@ def tile_chebyshev_l3_sparsed32_stack_pb_t_kernel(tc, z, T3, mask, x1, x2, C_w, 
                     xh = psum.tile([P, 2, P], F32, name="xh", tag="p3", bufs=4)
                     for u in range(2):
                         nc.tensor.transpose(xh[:, u, :], x_words(k, unit, g, u), ident_f[:])
-                    if g == 0:
-                        nc.scalar.copy(out=dst[:, unit, g], in_=xh[:].rearrange("p u b -> p b u"))
-                    else:
-                        nc.vector.tensor_copy(out=dst[:, unit, g], in_=xh[:].rearrange("p u b -> p b u"))
+                    nc.scalar.copy(out=dst[:, unit, g], in_=xh[:].rearrange("p u b -> p b u"))
             else:
                 xt = psum.tile([P, 4, P], F32, name="xt", tag=bank[0], bufs=bank[1])
                 for g in range(2):
@@ -400,18 +397,21 @@ def tile_chebyshev_l3_sparsed32_stack_pb_t_kernel(tc, z, T3, mask, x1, x2, C_w, 
 
         for k in range(NPAIR):
             last = k == NPAIR - 1
+            if k + 7 < NPAIR:
+                load_z(k + 7)
             if k + 5 < NPAIR:
                 load_x2(k + 5)
                 load_x1(k + 5)
-            if k + 7 < NPAIR:
-                load_z(k + 7)
             op1(k, 0)
-            mm1(k, 3)
+            if k > 0:
+                mm1(k, 3)
             if k >= 5:
                 mm2_t(k - 5)
             if k + 2 < NPAIR:
                 z_t(k + 2, 0)
                 z_t(k + 2, 1)
+                if k == 0:
+                    mm1(0, 3)
             else:
                 x_t(k - 2, 0)
                 x_t(k - 2, 1)
@@ -432,12 +432,11 @@ def tile_chebyshev_l3_sparsed32_stack_pb_t_kernel(tc, z, T3, mask, x1, x2, C_w, 
                 op2_bank(k - 1, 0)
                 x1_bank(k - 1, 1)
             op1(k, 2)
-            op1(k, 3, GATE_GROUPS, 32)
             if last:
-                for i in range(1, 4):
-                    x1_end(k, i)
-            if last:
+                op1(k, 3)
                 mm2_t(k - 4, P3_BANK)
+            else:
+                op1(k, 3, GATE_GROUPS, 32)
             if k >= 5:
                 out_t(k - 5)
             if 2 <= k < NPAIR - 2:
@@ -465,11 +464,11 @@ def tile_chebyshev_l3_sparsed32_stack_pb_t_kernel(tc, z, T3, mask, x1, x2, C_w, 
                 elif 0 < k and k + 2 < NPAIR:
                     z_q(k + 2)
                 op2(k, 0, GP_GROUPS, nc.gpsimd)
-            else:
-                op1(k, 3, 0, GATE_GROUPS)
 
         e = NPAIR - 1
         op2(e, 0, 8, nc.gpsimd)
+        for i in range(1, 4):
+            x1_end(e, i)
         out_t(e - 4)
         x_t(e - 1, 0)
         x_t(e - 1, 1)

@@ -18,7 +18,6 @@ NPAIR = 16
 FLOPS = 2 * B * KIN * F + 2 * B * F * O
 
 GP_GROUPS = 20
-PS_RANGES = [(20, 28), (28, 32)]
 GATE_GROUPS = 8
 VECTOR_BIAS = 12
 WARM = 512
@@ -114,14 +113,33 @@ def tile_chebyshev_l3_sparsed32_stack_pb_t_kernel(tc, z, T3, mask, x1, x2, C_w, 
             for i in range(times):
                 nc.tensor.matmul(out=bank, lhsT=still[:, 0:P], rhs=still[:], start=True, stop=True)
 
+        q_in = {}
+        q_codes = {}
+        q_scales = {}
+        QW = 2048
+
+        def place(j, half):
+            if j not in q_in:
+                q_in[j] = work.tile([P, 2 * QW], BF16, name="q_in_%d" % (j + 2), tag="q_in", bufs=3, align_bytes=64)
+            return q_in[j][:, half * QW:(half + 1) * QW]
+
+        def quantise(j, lo, n):
+            if j not in q_codes:
+                q_codes[j] = work.tile([P, QW // 2], U32, name="q_codes_%d" % (j + 2), tag="q_codes", bufs=4, align_bytes=64)
+                q_scales[j] = work.tile([P, QW // 2], U8, name="q_scales_%d" % (j + 2), tag="q_scales", bufs=4, align_bytes=64)
+            nc.vector.quantize_mx(
+                out=q_codes[j][:, lo // 4:(lo + n) // 4].bitcast(FP8X4), scales=q_scales[j][:, lo // 4:(lo + n) // 4],
+                in_=q_in[j][:, lo:lo + n])
+
         zg = {}
         zp = {}
-        zc = {}
-        zs = {}
+
+        def z_codes(k, lo):
+            return q_codes[k - 2][:, lo:lo + P].bitcast(FP8X4), q_scales[k - 2][:, lo:lo + P]
 
         def z_t(k, g):
             if g == 0:
-                zg[k] = work.tile([P, 2 * 256 * 4], BF16, name="zg_%d" % k, tag="zg", align_bytes=64)
+                zg[k] = place(k - 2, 0)
             zw = zp[k][:] if k in zp else z_sb[k].bitcast(F32)
             zt = psum.tile([P, 2, 256], F32, name="zt", tag="tt", bufs=2)
             for u in range(2):
@@ -129,18 +147,13 @@ def tile_chebyshev_l3_sparsed32_stack_pb_t_kernel(tc, z, T3, mask, x1, x2, C_w, 
                     col = jl * 512 + 256 * g
                     words = zw[:, col + u * P:col + (u + 1) * P] if k in zp else zw[:, col + u:col + 256:2]
                     nc.tensor.transpose(zt[:, u, jl * P:(jl + 1) * P], words, ident_f[:])
-            zgw = zg[k][:].bitcast(F32).rearrange("p (g c u) -> p g c u", g=2, u=2)
+            zgw = zg[k].bitcast(F32).rearrange("p (g c u) -> p g c u", g=2, u=2)
             nc.scalar.copy(out=zgw[:, g, :, :], in_=zt[:].rearrange("p u c -> p c u"))
 
         def z_perm(k):
             zp[k] = work.tile([P, KIN], F32, name="zp_%d" % k, tag="zp", bufs=2)
             nc.scalar.copy(out=zp[k][:].rearrange("p (a u w) -> p a u w", u=2, w=P),
                            in_=z_sb[k].bitcast(F32).rearrange("p (a w u) -> p a u w", u=2, w=P))
-
-        def z_q(k):
-            zc[k] = work.tile([P, 512], U32, name="zc_%d" % k, tag="zc", bufs=4, align_bytes=64)
-            zs[k] = work.tile([P, 512], U8, name="zs_%d" % k, tag="zs", bufs=4, align_bytes=64)
-            nc.vector.quantize_mx(out=zc[k][:].bitcast(FP8X4), scales=zs[k][:], in_=zg[k][:])
 
         wg = const.tile([P, 8 * 256 * 4], BF16, name="wg", align_bytes=64)
         wc = const.tile([P, 8 * 256], U32, name="wc", align_bytes=64)
@@ -217,9 +230,16 @@ def tile_chebyshev_l3_sparsed32_stack_pb_t_kernel(tc, z, T3, mask, x1, x2, C_w, 
         y_sb = {}
         x3_sb = {}
         xg = {}
-        xc = {}
-        xs = {}
         po = {}
+
+        def x_place(k):
+            return {12: (14, 0), 13: (15, 0), 14: (15, 1), 15: (16, 0)}.get(k, (k + 3, 1))
+
+        def x_codes(k, lo, n):
+            j, half = x_place(k)
+            cols = slice(half * 512 + lo, half * 512 + lo + n)
+            return q_codes[j][:, cols].bitcast(FP8X4), q_scales[j][:, cols]
+
 
         def mm1(k, pr):
             bank = psum.tile([P, 512], F32, name="p3_%d_%d" % (k, pr), tag="p3", bufs=4)
@@ -229,9 +249,9 @@ def tile_chebyshev_l3_sparsed32_stack_pb_t_kernel(tc, z, T3, mask, x1, x2, C_w, 
                 for g in gs:
                     lo = g * 256 + jl * P
                     ci = CI[(pr, g)]
+                    codes, scales = z_codes(k, lo)
                     nc.tensor.matmul_mx(
-                        out=bank[:, jl * 256:(jl + 1) * 256],
-                        lhsT=zc[k][:, lo:lo + P].bitcast(FP8X4), lhsT_scale=zs[k][:, lo:lo + P],
+                        out=bank[:, jl * 256:(jl + 1) * 256], lhsT=codes, lhsT_scale=scales,
                         rhs=wc[:, ci * 256:(ci + 1) * 256].bitcast(FP8X4), rhs_scale=ws[:, ci * 256:(ci + 1) * 256],
                         start=(g == gs[0]), stop=(g == gs[-1]))
 
@@ -262,13 +282,17 @@ def tile_chebyshev_l3_sparsed32_stack_pb_t_kernel(tc, z, T3, mask, x1, x2, C_w, 
 
         xb = {}
 
+        def ps_range(k, i):
+            lo = GP_GROUPS
+            return [(lo, lo + 8), (lo + 8, 32)][i]
+
         def x1_bank(k, i):
-            lo, hi = PS_RANGES[i]
+            lo, hi = ps_range(k, i)
             xb[k] = psum.tile([P, 64 * (hi - lo)], F32, name="xb_%d" % i, tag="xb", bufs=1)
             nc.tensor.matmul(out=xb[k][:], lhsT=ident_b[:], rhs=x1_sb[k][:, 64 * lo:64 * hi], start=True, stop=True)
 
         def op2_bank(k, i):
-            lo, hi = PS_RANGES[i]
+            lo, hi = ps_range(k, i)
             subtract(k, lo, hi, xb[k][:], nc.vector)
 
         xe = {}
@@ -286,8 +310,8 @@ def tile_chebyshev_l3_sparsed32_stack_pb_t_kernel(tc, z, T3, mask, x1, x2, C_w, 
 
         def x_t(k, unit, bank=("tt", 2), split=False):
             if unit == 0:
-                xg[k] = work.tile([P, 2 * 1024], BF16, name="xg_%d" % k, tag="xg", bufs=3, align_bytes=64)
-            words = xg[k][:].bitcast(F32)
+                xg[k] = place(*x_place(k))
+            words = xg[k].bitcast(F32)
             if k < VECTOR_BIAS:
                 dst = words.rearrange("p (g v b u) -> p v g b u", v=2, g=2, u=2)
             else:
@@ -306,22 +330,17 @@ def tile_chebyshev_l3_sparsed32_stack_pb_t_kernel(tc, z, T3, mask, x1, x2, C_w, 
                 nc.scalar.copy(out=dst[:, unit], in_=xt[:].rearrange("p (g u) b -> p g b u", u=2))
 
         def x_q(k, units):
-            if k not in xc:
-                xc[k] = work.tile([P, 512], U32, name="xc_%d" % k, tag="xc", align_bytes=64)
-                xs[k] = work.tile([P, 512], U8, name="xs_%d" % k, tag="xs", align_bytes=64)
-            lo, n = units[0] * 256, len(units) * 256
-            nc.vector.quantize_mx(
-                out=xc[k][:, lo:lo + n].bitcast(FP8X4), scales=xs[k][:, lo:lo + n], in_=xg[k][:, 4 * lo:4 * (lo + n)])
+            j, half = x_place(k)
+            quantise(j, half * QW + units[0] * 1024, len(units) * 1024)
 
         def mm2(k, units, bank=("po", 1)):
             key = (k, units[0])
             po[key] = psum.tile([P, len(units), O], F32, name="po_%d_%d" % key, tag=bank[0], bufs=bank[1])
             for i, unit in enumerate(units):
                 for g in range(2):
-                    lo = (unit * 2 + g) * P
+                    codes, scales = x_codes(k, (unit * 2 + g) * P, P)
                     nc.tensor.matmul_mx(
-                        out=po[key][:, i, :],
-                        lhsT=xc[k][:, lo:lo + P].bitcast(FP8X4), lhsT_scale=xs[k][:, lo:lo + P],
+                        out=po[key][:, i, :], lhsT=codes, lhsT_scale=scales,
                         rhs=cc[:, g * O:(g + 1) * O].bitcast(FP8X4), rhs_scale=cs[:, g * O:(g + 1) * O],
                         start=(g == 0), stop=(g == 1))
 
@@ -331,10 +350,11 @@ def tile_chebyshev_l3_sparsed32_stack_pb_t_kernel(tc, z, T3, mask, x1, x2, C_w, 
         def mm2_t(k, bank=("po", 1)):
             pt[k] = psum.tile([P, 2, 256], F32, name="pt_%d" % k, tag=bank[0], bufs=bank[1])
             for g in range(2):
+                codes, scales = x_codes(k, 256 * g, 256)
                 nc.tensor.matmul_mx(
                     out=pt[k][:, 0, :],
                     lhsT=cc[:, g * O:(g + 1) * O].bitcast(FP8X4), lhsT_scale=cs[:, g * O:(g + 1) * O],
-                    rhs=xc[k][:, 256 * g:256 * (g + 1)].bitcast(FP8X4), rhs_scale=xs[k][:, 256 * g:256 * (g + 1)],
+                    rhs=codes, rhs_scale=scales,
                     start=(g == 0), stop=(g == 1))
             ot[k] = work.tile([P, 256], F32, name="ot_%d" % k, tag="ot", bufs=2)
             nc.scalar.activation(out=ot[k][:], in_=pt[k][:, 0, :], func=ACTF.Identity, bias=bias_col[:, 0:1], scale=1.0)
@@ -384,7 +404,7 @@ def tile_chebyshev_l3_sparsed32_stack_pb_t_kernel(tc, z, T3, mask, x1, x2, C_w, 
         z_t(0, 0)
         z_t(0, 1)
         w_t(3)
-        z_q(0)
+        quantise(-2, 0, QW)
         w_mul(3, 0)
         w_mul(3, 1)
         w_q(2, [0])
@@ -394,6 +414,9 @@ def tile_chebyshev_l3_sparsed32_stack_pb_t_kernel(tc, z, T3, mask, x1, x2, C_w, 
         w_q(2, [1, 2, 3])
         for pr in range(1, 3):
             mm1(0, pr)
+
+        def joint(k):
+            return 5 <= k <= 13
 
         for k in range(NPAIR):
             last = k == NPAIR - 1
@@ -421,21 +444,19 @@ def tile_chebyshev_l3_sparsed32_stack_pb_t_kernel(tc, z, T3, mask, x1, x2, C_w, 
                 z_perm(k + 3)
             if k == 0:
                 op1(k, 1)
-                z_q(1)
-            if not last:
-                mm1(k + 1, 0)
-            if k > 0:
-                op1(k, 1)
-            if not last:
-                mm1(k + 1, 1)
+                quantise(-1, 0, QW)
             if k >= 1:
                 op2_bank(k - 1, 0)
                 x1_bank(k - 1, 1)
+                op1(k, 1)
+            if not last:
+                mm1(k + 1, 0)
+                mm1(k + 1, 1)
             op1(k, 2)
             if last:
                 op1(k, 3)
                 mm2_t(k - 4, P3_BANK)
-            else:
+            elif not joint(k):
                 op1(k, 3, GATE_GROUPS, 32)
             if k >= 5:
                 out_t(k - 5)
@@ -446,23 +467,24 @@ def tile_chebyshev_l3_sparsed32_stack_pb_t_kernel(tc, z, T3, mask, x1, x2, C_w, 
                 c_t()
             if k == 4:
                 bias_spread()
-            if not last:
-                mm1(k + 1, 2)
             if k >= 1:
                 op2_bank(k - 1, 1)
             if not last:
                 x1_bank(k, 0)
+                mm1(k + 1, 2)
                 if k == 4:
                     c_q()
-                if k >= 3:
-                    x_q(k - 3, BOTH)
-                if k == 0:
-                    z_q(2)
-                op1(k, 3, 0, GATE_GROUPS)
-                if k == NPAIR - 2:
-                    x_q(k - 2, BOTH)
-                elif 0 < k and k + 2 < NPAIR:
-                    z_q(k + 2)
+                if joint(k):
+                    op1(k, 3)
+                    quantise(k, 0, 2 * QW)
+                else:
+                    if k >= 3:
+                        quantise(k, QW, QW)
+                    if k == 0:
+                        quantise(k, 0, QW)
+                    op1(k, 3, 0, GATE_GROUPS)
+                    if k > 0:
+                        quantise(k, 0, QW)
                 op2(k, 0, GP_GROUPS, nc.gpsimd)
 
         e = NPAIR - 1

from contextlib import ExitStack

import concourse.mybir as mybir
from concourse.masks import make_identity

F32 = mybir.dt.float32
BF16 = mybir.dt.bfloat16
U32 = mybir.dt.uint32
U8 = mybir.dt.uint8
FP8X4 = mybir.dt.float8_e4m3fn_x4
ALU = mybir.AluOpType
ACTF = mybir.ActivationFunctionType

P = 128
B, KIN, F, O = 4096, 1024, 1024, 128
NCH = 8
NPAIR = 16
FLOPS = 2 * B * KIN * F + 2 * B * F * O

GP_GROUPS = 20
GATE_GROUPS = 8
VECTOR_BIAS = 12
WARM = 512
G_OF_PR = [[0], [0, 1], [0, 1], [1]]
CI = {(0, 0): 0, (1, 0): 1, (2, 0): 2, (1, 1): 5, (2, 1): 6, (3, 1): 7}


def tile_chebyshev_l3_sparsed32_stack_pb_t_kernel(tc, z, T3, mask, x1, x2, C_w, C_b, out):
    nc = tc.nc
    with ExitStack() as ctx:
        const = ctx.enter_context(tc.tile_pool(name="const", bufs=1))
        stream = ctx.enter_context(tc.tile_pool(name="stream", bufs=8))
        work = ctx.enter_context(tc.tile_pool(name="work", bufs=3))
        psum = ctx.enter_context(tc.psum_pool(name="psum", bufs=1))
        ctx.enter_context(tc.manual_schedule())

        zv = z.rearrange("(c p j) k -> c p (j k)", p=P, j=4)
        x1v = x1.rearrange("(c p j) k -> c p (j k)", p=P, j=4)
        x2v = x2.rearrange("(c p j) k -> c p (j k)", p=P, j=4)
        outv = out.rearrange("(c p j) o -> c p (j o)", p=P, j=4)
        t3v = T3.rearrange("(ft q) k -> q ft k", q=P)

        ident_f = const.tile([P, P], F32, name="ident_f")
        make_identity(nc, ident_f[:])

        ident_b = const.tile([P, P], BF16, name="ident_b")
        make_identity(nc, ident_b[:])
        PW = 2 * KIN
        z_sb = {}
        x1_sb = {}
        x2_sb = {}

        def load(dst, src, k, tag):
            t = stream.tile([P, PW], BF16, name="%s_%d" % (tag, k), tag=tag)
            nc.sync.dma_start(out=t[:], in_=src[k // 2][:, (k % 2) * PW:(k % 2 + 1) * PW])
            dst[k] = t[:]

        def load_z(k):
            load(z_sb, zv, k, "z")

        def load_x1(k):
            load(x1_sb, x1v, k, "x1")

        def load_x2(k):
            load(x2_sb, x2v, k, "x2")

        still = const.tile([P, WARM], BF16, name="still")
        nc.vector.memset(still[:], 0.0)
        mk_sb = const.tile([P, KIN // 2], BF16, name="mk_sb")
        nc.sync.dma_start(out=mk_sb[:], in_=mask[0:64, :].rearrange("c (g k) -> (c g) k", g=2))
        t3h = []
        for hh in range(2):
            t3_t = work.tile([P, 4 * KIN], BF16, name="t3_%d" % hh, tag="y", bufs=2)
            t3h.append(t3_t)

        def load_t3(fp):
            hh, lo = fp // 2, (fp % 2) * 2 * KIN
            nc.sync.dma_start(
                out=t3h[hh][:, lo:lo + 2 * KIN].rearrange("p (f k) -> p f k", f=2),
                in_=t3v[:, 2 * fp:2 * fp + 2, :])

        for fp in range(3):
            load_t3(fp)
        c_sb = const.tile([P, F], BF16, name="c_sb")
        ones = const.tile([P, P], BF16, name="ones")
        nc.gpsimd.memset(ones[:], 1.0)
        bias_row = const.tile([P, O], BF16, name="bias_row")
        nc.gpsimd.memset(bias_row[:], 0.0)
        bias_sb = const.tile([P, O], F32, name="bias_sb")
        bias_col = const.tile([P, 2], F32, name="bias_col")
        load_z(0)
        load_t3(3)
        load_z(1)
        load_x2(0)
        load_z(2)
        load_x1(0)
        load_x2(1)
        load_z(3)
        load_x2(2)
        load_x1(1)
        load_z(4)
        load_x2(3)
        load_x1(2)
        nc.sync.dma_start(out=c_sb[:], in_=C_w)
        nc.sync.dma_start(out=bias_row[0:1, :], in_=C_b.unsqueeze(0))
        load_z(5)
        load_x2(4)
        load_x1(3)
        load_z(6)
        load_x1(4)

        def busy(bank, times=1):
            for i in range(times):
                nc.tensor.matmul(out=bank, lhsT=still[:, 0:P], rhs=still[:], start=True, stop=True)

        q_in = {}
        q_codes = {}
        q_scales = {}
        QW = 2048

        def place(j, half):
            if j not in q_in:
                q_in[j] = work.tile([P, 2 * QW], BF16, name="q_in_%d" % (j + 2), tag="q_in", bufs=3, align_bytes=64)
            return q_in[j][:, half * QW:(half + 1) * QW]

        def quantise(j, lo, n):
            if j not in q_codes:
                q_codes[j] = work.tile([P, QW // 2], U32, name="q_codes_%d" % (j + 2), tag="q_codes", bufs=4, align_bytes=64)
                q_scales[j] = work.tile([P, QW // 2], U8, name="q_scales_%d" % (j + 2), tag="q_scales", bufs=4, align_bytes=64)
            nc.vector.quantize_mx(
                out=q_codes[j][:, lo // 4:(lo + n) // 4].bitcast(FP8X4), scales=q_scales[j][:, lo // 4:(lo + n) // 4],
                in_=q_in[j][:, lo:lo + n])

        zg = {}
        zp = {}

        def z_codes(k, lo):
            return q_codes[k - 2][:, lo:lo + P].bitcast(FP8X4), q_scales[k - 2][:, lo:lo + P]

        def z_t(k, g):
            if g == 0:
                zg[k] = place(k - 2, 0)
            zw = zp[k][:] if k in zp else z_sb[k].bitcast(F32)
            zt = psum.tile([P, 2, 256], F32, name="zt", tag="tt", bufs=2)
            for u in range(2):
                for jl in range(2):
                    col = jl * 512 + 256 * g
                    words = zw[:, col + u * P:col + (u + 1) * P] if k in zp else zw[:, col + u:col + 256:2]
                    nc.tensor.transpose(zt[:, u, jl * P:(jl + 1) * P], words, ident_f[:])
            zgw = zg[k].bitcast(F32).rearrange("p (g c u) -> p g c u", g=2, u=2)
            nc.scalar.copy(out=zgw[:, g, :, :], in_=zt[:].rearrange("p u c -> p c u"))

        def z_perm(k):
            zp[k] = work.tile([P, KIN], F32, name="zp_%d" % k, tag="zp", bufs=2)
            nc.scalar.copy(out=zp[k][:].rearrange("p (a u w) -> p a u w", u=2, w=P),
                           in_=z_sb[k].bitcast(F32).rearrange("p (a w u) -> p a u w", u=2, w=P))

        wg = const.tile([P, 8 * 256 * 4], BF16, name="wg", align_bytes=64)
        wc = const.tile([P, 8 * 256], U32, name="wc", align_bytes=64)
        ws = const.tile([P, 8 * 256], U8, name="ws", align_bytes=64)
        wgw = wg[:].bitcast(F32).rearrange("p (g pr s r u) -> p g s pr r u", g=2, pr=4, s=16, r=16, u=2)
        wgv = wg[:].rearrange("p (g pr s q) -> p g pr s q", g=2, pr=4, s=16, q=64)
        PR_OF_G = [slice(0, 3), slice(1, 4)]

        mt = const.tile([P, 2 * 64 * 4], BF16, name="mt", align_bytes=64)
        mtv = mt[:].rearrange("p (g pr q) -> p g pr q", g=2, pr=4)

        def mask_t():
            mw = mk_sb[:].bitcast(F32)
            mb = psum.tile([P, 2, P], F32, name="mb", tag="tt", bufs=2)
            for u in range(2):
                nc.tensor.transpose(mb[:, u, :], mw[:, u:256:2], ident_f[:])
            nc.scalar.copy(out=mt[:].bitcast(F32).rearrange("p (g c u) -> p g c u", g=2, u=2),
                           in_=mb[:].rearrange("p u (c g) -> p g c u", g=2))

        def w_t(fp):
            tw = t3h[fp // 2][:].bitcast(F32)
            for g in range(2):
                wt = psum.tile([P, 2, 256], F32, name="wt", tag="p3", bufs=4)
                for u in range(2):
                    for fl in range(2):
                        first = ((fp % 2) * 2 + fl) * 512 + 256 * g
                        nc.tensor.transpose(wt[:, u, fl * P:(fl + 1) * P], tw[:, first + u:first + 256:2], ident_f[:])
                src = wt[:].rearrange("p u (s pr r) -> p s pr r u", s=4, pr=4, r=16)
                nc.scalar.copy(out=wgw[:, g, 4 * fp:4 * fp + 4, PR_OF_G[g], :, :], in_=src[:, :, PR_OF_G[g], :, :])

        def w_mul(fp, g):
            part = wgv[:, g, PR_OF_G[g], 4 * fp:4 * fp + 4, :]
            nc.vector.tensor_tensor(
                out=part, in0=part, in1=mtv[:, g, PR_OF_G[g], :].unsqueeze(2).to_broadcast([P, 3, 4, 64]), op=ALU.mult)

        def w_q(fp, prs):
            for pr in prs:
                for g in G_OF_PR[pr]:
                    lo_w = CI[(pr, g)] * 256 + 64 * fp
                    nc.vector.quantize_mx(
                        out=wc[:, lo_w:lo_w + 128].bitcast(FP8X4), scales=ws[:, lo_w:lo_w + 128],
                        in_=wg[:, 4 * lo_w:4 * (lo_w + 128)])

        cg = const.tile([P, 2 * O * 4], BF16, name="cg", align_bytes=64)
        cc = const.tile([P, 2 * O], U32, name="cc", align_bytes=64)
        cs = const.tile([P, 2 * O], U8, name="cs", align_bytes=64)

        def bias_spread():
            bt = psum.tile([P, O + 2], F32, name="bt", tag="po", bufs=1)
            nc.tensor.matmul(out=bt[:, 0:O], lhsT=ones[:], rhs=bias_row[:], start=True, stop=True)
            nc.tensor.matmul(out=bt[:, O:O + 2], lhsT=bias_row[:], rhs=ones[:, 0:2], start=True, stop=True)
            nc.scalar.copy(out=bias_sb[:], in_=bt[:, 0:O])
            nc.scalar.copy(out=bias_col[:], in_=bt[:, O:O + 2])

        cw = const.tile([P, F // 2], F32, name="cw")

        def c_perm():
            nc.scalar.copy(out=cw[:].rearrange("p (pr s w) -> p pr s w", pr=4, w=8),
                           in_=c_sb[:].bitcast(F32).rearrange("p (s pr w) -> p pr s w", pr=4, w=8))

        def c_t():
            ct = psum.tile([P, 4, P], F32, name="ct", tag="po", bufs=1)
            for g in range(2):
                for u in range(2):
                    nc.tensor.transpose(ct[:, 2 * g + u, :], cw[:, (2 * g + u) * P:(2 * g + u + 1) * P], ident_f[:])
            nc.scalar.copy(
                out=cg[:].bitcast(F32).rearrange("p (g o u) -> p g o u", g=2, u=2),
                in_=ct[:].rearrange("p (g u) o -> p g o u", u=2))

        def c_q():
            nc.vector.quantize_mx(out=cc[:].bitcast(FP8X4), scales=cs[:], in_=cg[:])

        p3 = {}
        y_sb = {}
        x3_sb = {}
        xg = {}
        po = {}

        def x_place(k):
            return {12: (14, 0), 13: (15, 0), 14: (15, 1), 15: (16, 0)}.get(k, (k + 3, 1))

        def x_codes(k, lo, n):
            j, half = x_place(k)
            cols = slice(half * 512 + lo, half * 512 + lo + n)
            return q_codes[j][:, cols].bitcast(FP8X4), q_scales[j][:, cols]


        def mm1(k, pr):
            bank = psum.tile([P, 512], F32, name="p3_%d_%d" % (k, pr), tag="p3", bufs=4)
            p3[(k, pr)] = bank
            gs = G_OF_PR[pr]
            for jl in range(2):
                for g in gs:
                    lo = g * 256 + jl * P
                    ci = CI[(pr, g)]
                    codes, scales = z_codes(k, lo)
                    nc.tensor.matmul_mx(
                        out=bank[:, jl * 256:(jl + 1) * 256], lhsT=codes, lhsT_scale=scales,
                        rhs=wc[:, ci * 256:(ci + 1) * 256].bitcast(FP8X4), rhs_scale=ws[:, ci * 256:(ci + 1) * 256],
                        start=(g == gs[0]), stop=(g == gs[-1]))

        def op1(k, pr, lo=0, hi=32):
            if k not in y_sb:
                y_sb[k] = work.tile([P, PW], F32, name="y_%d" % k, tag="y", bufs=2)
            yv = y_sb[k][:].rearrange("p (pr s r) -> p pr s r", pr=4, r=16)
            x2u = x2_sb[k].rearrange("p (s q) -> p s q", q=64)
            nc.vector.scalar_tensor_tensor(
                out=yv[:, pr, lo:hi, :],
                in0=p3[(k, pr)][:].rearrange("p (s r) -> p s r", r=16)[:, lo:hi, :],
                scalar=2.0,
                in1=x2u[:, lo:hi, pr * 16:(pr + 1) * 16],
                op0=ALU.mult, op1=ALU.mult)

        def by_pr(view):
            return view.rearrange("p (s pr r) -> p pr s r", pr=4, r=16)

        def subtract(k, lo, hi, x1_view, eng):
            if k not in x3_sb:
                x3_sb[k] = work.tile([P, PW], BF16, name="x3_%d" % k, tag="x3", bufs=3)
            yv = y_sb[k][:].rearrange("p (pr s r) -> p pr s r", pr=4, r=16)
            xv = x3_sb[k][:].rearrange("p (pr s r) -> p pr s r", pr=4, r=16)
            eng.tensor_tensor(out=xv[:, :, lo:hi, :], in0=yv[:, :, lo:hi, :], in1=by_pr(x1_view), op=ALU.subtract)

        def op2(k, lo, hi, eng):
            subtract(k, lo, hi, x1_sb[k][:, 64 * lo:64 * hi], eng)

        xb = {}

        def ps_range(k, i):
            lo = GP_GROUPS
            return [(lo, lo + 8), (lo + 8, 32)][i]

        def x1_bank(k, i):
            lo, hi = ps_range(k, i)
            xb[k] = psum.tile([P, 64 * (hi - lo)], F32, name="xb_%d" % i, tag="xb", bufs=1)
            nc.tensor.matmul(out=xb[k][:], lhsT=ident_b[:], rhs=x1_sb[k][:, 64 * lo:64 * hi], start=True, stop=True)

        def op2_bank(k, i):
            lo, hi = ps_range(k, i)
            subtract(k, lo, hi, xb[k][:], nc.vector)

        xe = {}

        def x1_end(k, i):
            xe[i] = psum.tile([P, 512], F32, name="xe_%d" % i, tag="p3", bufs=4)
            nc.tensor.matmul(out=xe[i][:], lhsT=ident_b[:], rhs=x1_sb[k][:, 512 * i:512 * i + 512], start=True, stop=True)

        def op2_end(k, i):
            subtract(k, 8 * i, 8 * i + 8, xe[i][:], nc.vector)

        def x_words(k, unit, g, u):
            first = (2 * g + u) * 256 + unit * P
            return x3_sb[k][:].bitcast(F32)[:, first:first + P]

        def x_t(k, unit, bank=("tt", 2), split=False):
            if unit == 0:
                xg[k] = place(*x_place(k))
            words = xg[k].bitcast(F32)
            if k < VECTOR_BIAS:
                dst = words.rearrange("p (g v b u) -> p v g b u", v=2, g=2, u=2)
            else:
                dst = words.rearrange("p (v g b u) -> p v g b u", v=2, g=2, u=2)
            if split:
                for g in range(2):
                    xh = psum.tile([P, 2, P], F32, name="xh", tag="p3", bufs=4)
                    for u in range(2):
                        nc.tensor.transpose(xh[:, u, :], x_words(k, unit, g, u), ident_f[:])
                    nc.scalar.copy(out=dst[:, unit, g], in_=xh[:].rearrange("p u b -> p b u"))
            else:
                xt = psum.tile([P, 4, P], F32, name="xt", tag=bank[0], bufs=bank[1])
                for g in range(2):
                    for u in range(2):
                        nc.tensor.transpose(xt[:, 2 * g + u, :], x_words(k, unit, g, u), ident_f[:])
                nc.scalar.copy(out=dst[:, unit], in_=xt[:].rearrange("p (g u) b -> p g b u", u=2))

        def x_q(k, units):
            j, half = x_place(k)
            quantise(j, half * QW + units[0] * 1024, len(units) * 1024)

        def mm2(k, units, bank=("po", 1)):
            key = (k, units[0])
            po[key] = psum.tile([P, len(units), O], F32, name="po_%d_%d" % key, tag=bank[0], bufs=bank[1])
            for i, unit in enumerate(units):
                for g in range(2):
                    codes, scales = x_codes(k, (unit * 2 + g) * P, P)
                    nc.tensor.matmul_mx(
                        out=po[key][:, i, :], lhsT=codes, lhsT_scale=scales,
                        rhs=cc[:, g * O:(g + 1) * O].bitcast(FP8X4), rhs_scale=cs[:, g * O:(g + 1) * O],
                        start=(g == 0), stop=(g == 1))

        pt = {}
        ot = {}

        def mm2_t(k, bank=("po", 1)):
            pt[k] = psum.tile([P, 2, 256], F32, name="pt_%d" % k, tag=bank[0], bufs=bank[1])
            for g in range(2):
                codes, scales = x_codes(k, 256 * g, 256)
                nc.tensor.matmul_mx(
                    out=pt[k][:, 0, :],
                    lhsT=cc[:, g * O:(g + 1) * O].bitcast(FP8X4), lhsT_scale=cs[:, g * O:(g + 1) * O],
                    rhs=codes, rhs_scale=scales,
                    start=(g == 0), stop=(g == 1))
            ot[k] = work.tile([P, 256], F32, name="ot_%d" % k, tag="ot", bufs=2)
            nc.scalar.activation(out=ot[k][:], in_=pt[k][:, 0, :], func=ACTF.Identity, bias=bias_col[:, 0:1], scale=1.0)

        o_sb = {}

        def out_t(k):
            c = k // 2
            for unit in range(2):
                nc.tensor.transpose(pt[k][:, 1, unit * P:(unit + 1) * P], ot[k][:, unit * P:(unit + 1) * P], ident_f[:])
            if c not in o_sb:
                o_sb[c] = work.tile([P, 4, O], F32, name="o_sb_%d" % c, tag="o_sb", bufs=7)
            lo = (k % 2) * 2
            nc.scalar.copy(out=o_sb[c][:, lo:lo + 2, :].rearrange("p j o -> p (j o)"), in_=pt[k][:, 1, :])
            if k % 2 == 1:
                nc.sync.dma_start(out=outv[c], in_=o_sb[c][:].rearrange("p j o -> p (j o)"))

        def fin(k, units, store):
            c = k // 2
            if c not in o_sb:
                o_sb[c] = work.tile([P, 4, O], F32, name="o_sb_%d" % c, tag="o_sb", bufs=7)
            lo, n = (k % 2) * 2 + units[0], len(units)
            nc.vector.tensor_tensor(
                out=o_sb[c][:, lo:lo + n, :], in0=po[(k, units[0])][:],
                in1=bias_sb[:].unsqueeze(1).to_broadcast([P, n, O]), op=ALU.add)
            if store:
                first = lo + n - store
                nc.sync.dma_start(out=outv[c][:, first * O:(lo + n) * O],
                                  in_=o_sb[c][:, first:lo + n, :].rearrange("p j o -> p (j o)"))

        BOTH = [0, 1]

        P3_BANK = ("p3", 4)
        warm_bank = psum.tile([P, WARM], F32, name="warm_bank", tag="po", bufs=1)
        busy(warm_bank[:], 5)
        mask_t()
        w_t(0)
        w_mul(0, 0)
        w_mul(0, 1)
        w_t(1)
        w_mul(1, 0)
        w_mul(1, 1)
        w_t(2)
        w_q(0, range(4))
        w_mul(2, 0)
        w_mul(2, 1)
        z_t(0, 0)
        z_t(0, 1)
        w_t(3)
        quantise(-2, 0, QW)
        w_mul(3, 0)
        w_mul(3, 1)
        w_q(2, [0])
        z_t(1, 0)
        z_t(1, 1)
        mm1(0, 0)
        w_q(2, [1, 2, 3])
        for pr in range(1, 3):
            mm1(0, pr)

        def joint(k):
            return 5 <= k <= 13

        for k in range(NPAIR):
            last = k == NPAIR - 1
            if k + 7 < NPAIR:
                load_z(k + 7)
            if k + 5 < NPAIR:
                load_x2(k + 5)
                load_x1(k + 5)
            op1(k, 0)
            if k > 0:
                mm1(k, 3)
            if k >= 5:
                mm2_t(k - 5)
            if k + 2 < NPAIR:
                z_t(k + 2, 0)
                z_t(k + 2, 1)
                if k == 0:
                    mm1(0, 3)
            else:
                x_t(k - 2, 0)
                x_t(k - 2, 1)
            if k == 2:
                c_perm()
            if 4 <= k and k + 3 < NPAIR:
                z_perm(k + 3)
            if k == 0:
                op1(k, 1)
                quantise(-1, 0, QW)
            if k >= 1:
                op2_bank(k - 1, 0)
                x1_bank(k - 1, 1)
                op1(k, 1)
            if not last:
                mm1(k + 1, 0)
                mm1(k + 1, 1)
            op1(k, 2)
            if last:
                op1(k, 3)
                mm2_t(k - 4, P3_BANK)
            elif not joint(k):
                op1(k, 3, GATE_GROUPS, 32)
            if k >= 5:
                out_t(k - 5)
            if 2 <= k < NPAIR - 2:
                x_t(k - 2, 0)
                x_t(k - 2, 1)
            if k == 3:
                c_t()
            if k == 4:
                bias_spread()
            if k >= 1:
                op2_bank(k - 1, 1)
            if not last:
                x1_bank(k, 0)
                mm1(k + 1, 2)
                if k == 4:
                    c_q()
                if joint(k):
                    op1(k, 3)
                    quantise(k, 0, 2 * QW)
                else:
                    if k >= 3:
                        quantise(k, QW, QW)
                    if k == 0:
                        quantise(k, 0, QW)
                    op1(k, 3, 0, GATE_GROUPS)
                    if k > 0:
                        quantise(k, 0, QW)
                op2(k, 0, GP_GROUPS, nc.gpsimd)

        e = NPAIR - 1
        op2(e, 0, 8, nc.gpsimd)
        for i in range(1, 4):
            x1_end(e, i)
        out_t(e - 4)
        x_t(e - 1, 0)
        x_t(e - 1, 1)
        mm2(e - 3, BOTH)
        for i in range(1, 4):
            op2_end(e, i)
        x_q(e - 2, BOTH)
        fin(e - 3, BOTH, 0)
        x_t(e, 0, P3_BANK)
        x_t(e, 1, P3_BANK, True)
        mm2(e - 2, BOTH)
        x_q(e - 1, BOTH)
        fin(e - 2, BOTH, 4)
        x_q(e, [0])
        mm2(e - 1, BOTH, P3_BANK)
        mm2(e, [0], P3_BANK)
        x_q(e, [1])
        fin(e - 1, BOTH, 2)
        mm2(e, [1], P3_BANK)
        fin(e, [0], 1)
        fin(e, [1], 1)
